import numpy as np
import ml_dtypes


def mxq(x, axis, fmt="e4m3"):
    dtype, down = {"e4m3": (ml_dtypes.float8_e4m3fn, 7), "e5m2": (ml_dtypes.float8_e5m2, 14)}[fmt]
    v = np.moveaxis(np.asarray(x, np.float32).astype(ml_dtypes.bfloat16).astype(np.float64), axis, -1)
    blocks = v.reshape(v.shape[:-1] + (-1, 32))
    amax = np.abs(blocks).max(-1, keepdims=True)
    byte = np.maximum(np.where(amax > 0, np.frexp(amax)[1] - 1 + 127, 0) - down, 1)
    scale = np.exp2(byte - 127.0)
    codes = (blocks / scale).astype(np.float32).astype(dtype).astype(np.float64)
    return np.moveaxis((codes * scale).reshape(v.shape), -1, axis)


WIDE = False


def mx_kscale(k):
    if not WIDE:
        return np.ones(k)
    levels = np.array([10, -10, 5, -5, 0])
    a = np.random.permutation(np.resize(levels, k // 512 * 4)).reshape(k // 512, 4)
    idx = np.arange(k)
    return np.exp2(a[idx // 512, idx % 128 // 32])


BF16 = ml_dtypes.bfloat16


def bf(x):
    return np.asarray(x, np.float32).astype(BF16)


def f64(x):
    return np.asarray(x).astype(np.float64)


B, C, H, W, HID, D, K = 2, 1536, 32, 32, 512, 128, 64
N = H * W
ITERS = 3


def lse(a, axis):
    m = a.max(axis=axis, keepdims=True)
    return np.squeeze(m, axis=axis) + np.log(np.exp(a - m).sum(axis=axis))


def sinkhorn_log(S, num_iters=ITERS):
    b, m, n = S.shape
    norm = -np.log(float(n))
    log_a = np.full((b, m), norm)
    log_b = np.full((b, n), norm)
    u = np.zeros((b, m))
    v = np.zeros((b, n))
    for _ in range(num_iters):
        u = log_a - lse(S + v[:, None, :], 2)
        v = log_b - lse(S + u[:, :, None], 1)
    return S + u[:, :, None] + v[:, None, :] - norm


def setup_inputs():
    t = mx_kscale(HID)
    return {
        "h_cluster": bf(np.maximum(np.random.standard_normal((B, HID, N)), 0.0) * t[None, :, None]),
        "w2c": bf(np.random.standard_normal((D, HID)) / np.sqrt(HID) / t[None, :]),
        "b2c": bf(np.random.standard_normal(D) * 0.1),
        "scores": bf(np.random.standard_normal((B, K, N)) * 2.0),
        "temperature": bf(np.atleast_1d(1.5 + 0.1 * np.random.standard_normal())),
    }


def reference(h_cluster, w2c, b2c, scores, temperature):
    f = (mxq(f64(w2c), 1, "e4m3") @ mxq(f64(h_cluster), 1, "e4m3")) + f64(b2c)[None, :, None]
    log_p = sinkhorn_log(f64(scores))
    p = np.exp(log_p / f64(temperature)) + np.exp(log_p)
    agg = mxq(f, 2, "e4m3") @ mxq(p, 2, "e4m3").transpose(0, 2, 1)
    flat = agg.reshape(agg.shape[0], -1)
    nrm = np.maximum(np.sqrt((flat ** 2).sum(-1, keepdims=True)), 1e-12)
    return flat / nrm

@@ -1,0 +1,287 @@
+from contextlib import ExitStack
+
+import concourse.mybir as mybir
+from concourse.masks import make_identity
+
+F32 = mybir.dt.float32
+BF16 = mybir.dt.bfloat16
+U32 = mybir.dt.uint32
+U8 = mybir.dt.uint8
+FP8X4 = mybir.dt.float8_e4m3fn_x4
+ALU = mybir.AluOpType
+ACT = mybir.ActivationFunctionType
+AXIS_X = mybir.AxisListType.X
+
+P = 128
+PACK = 4
+B, HID, N, D, K = 2, 512, 1024, 128, 64
+BK = B * K
+CHUNKS = N // P
+PASSES = N // (P * PACK)
+ROUNDS = 3
+
+FLOPS = 2 * B * (D * HID * N + D * K * N)
+
+
+def tile_image_aggregation_pa_s_kernel(tc, h_cluster, w2c, b2c, scores, temperature, out):
+    nc = tc.nc
+    with ExitStack() as ctx:
+        keep = ctx.enter_context(tc.tile_pool(name="keep", bufs=1))
+        banks = ctx.enter_context(tc.psum_pool(name="banks", bufs=4))
+        vecs = ctx.enter_context(tc.psum_pool(name="vecs", bufs=3))
+        lone = ctx.enter_context(tc.psum_pool(name="lone", bufs=1))
+
+        ident = keep.tile([P, P], F32)
+        make_identity(nc, ident[:])
+        ones = keep.tile([P, P], F32)
+        nc.gpsimd.memset(ones[:], 1.0)
+        own_image = keep.tile([P, B], F32)
+        nc.vector.memset(own_image[:], 0.0)
+        for b in range(B):
+            nc.vector.memset(own_image[b * K : (b + 1) * K, b : b + 1], 1.0)
+
+        s_rows = keep.tile([P, N], BF16)
+        nc.sync.dma_start(out=s_rows[:], in_=scores.rearrange("b k n -> (b k) n"))
+        temp = keep.tile([P, 1], BF16)
+        nc.sync.dma_start(out=temp[:], in_=temperature.partition_broadcast(P))
+        w_rows = keep.tile([P, HID], BF16)
+        nc.sync.dma_start(out=w_rows[:], in_=w2c)
+        bias_rows = keep.tile([P, D], BF16)
+        nc.sync.dma_start(out=bias_rows[:], in_=b2c.partition_broadcast(P))
+        h_raw = keep.tile([P, B, PACK, N], BF16)
+        for b in range(B):
+            nc.sync.dma_start(out=h_raw[:, b], in_=h_cluster[b].rearrange("(p j) n -> p j n", j=PACK))
+
+        inv_temp = keep.tile([P, 1], F32)
+        nc.vector.reciprocal(out=inv_temp[:], in_=temp[:])
+
+        rowmax = keep.tile([P, 1], F32)
+        nc.vector.reduce_max(out=rowmax[:], in_=s_rows[:], axis=AXIS_X)
+        d_rows = keep.tile([P, N], F32)
+        colmax = keep.tile([P, CHUNKS, B], F32)
+        dm_cols = keep.tile([P, CHUNKS, BK], F32)
+        g_cols = keep.tile([P, CHUNKS, BK], F32)
+        gt_cols = keep.tile([P, CHUNKS, BK], F32)
+        g_rows = keep.tile([P, N], F32)
+        for g in range(PASSES):
+            pixels = slice(g * P * PACK, (g + 1) * P * PACK)
+            chunks = slice(g * PACK, (g + 1) * PACK)
+            nc.vector.tensor_scalar(
+                out=d_rows[:, pixels], in0=s_rows[:, pixels], scalar1=rowmax[:, 0:1], scalar2=None, op0=ALU.subtract
+            )
+            d_cols_ps = banks.tile([P, PACK, BK], F32, tag="bank")
+            for t in range(PACK):
+                c = g * PACK + t
+                nc.tensor.transpose(d_cols_ps[:, t, :], d_rows[:, c * P : (c + 1) * P], ident[:])
+            by_image = d_cols_ps[:].rearrange("p t (b k) -> p t b k", b=B)
+            nc.vector.tensor_reduce(out=colmax[:, chunks, :], in_=by_image, axis=AXIS_X, op=ALU.max)
+            nc.vector.tensor_tensor(
+                out=dm_cols[:, chunks, :].rearrange("p t (b k) -> p t b k", b=B),
+                in0=by_image,
+                in1=colmax[:, chunks, :].unsqueeze(3).to_broadcast([P, PACK, B, K]),
+                op=ALU.subtract,
+            )
+            nc.scalar.activation(out=g_cols[:, chunks, :], in_=dm_cols[:, chunks, :], func=ACT.Exp)
+
+        unused = keep.tile([P, N], BF16)
+        rowsum = keep.tile([P, 1], F32)
+        nc.scalar.activation(out=unused[:], in_=d_rows[:], func=ACT.Exp, accum_out=rowsum[:])
+
+        for g in range(PASSES):
+            pixels = slice(g * P * PACK, (g + 1) * P * PACK)
+            g_rows_ps = banks.tile([P, PACK, P], F32, tag="bank")
+            for t in range(PACK):
+                nc.tensor.transpose(g_rows_ps[:, t, :], g_cols[:, g * PACK + t, :], ident[:])
+            if g == 0:
+                nc.vector.tensor_copy(out=g_rows[:, pixels], in_=g_rows_ps[:].rearrange("p t n -> p (t n)"))
+            else:
+                nc.scalar.copy(out=g_rows[:, pixels], in_=g_rows_ps[:].rearrange("p t n -> p (t n)"))
+
+        nc.scalar.activation(out=gt_cols[:], in_=dm_cols[:], func=ACT.Exp, scale=inv_temp[:, 0:1])
+
+        a_vec = keep.tile([P, ROUNDS, B], F32)
+        b_vec = keep.tile([P, ROUNDS, CHUNKS, B], F32)
+        bcast_ps = None
+        a_col = keep.tile([P, 1], F32)
+        ln_a = keep.tile([P, 1], F32)
+        alpha_col = keep.tile([P, 1], F32)
+        for r in range(ROUNDS):
+            if r == 0:
+                nc.vector.reciprocal(out=a_col[:], in_=rowsum[:])
+                nc.vector.tensor_scalar(
+                    out=a_vec[:, r, :], in0=own_image[:], scalar1=a_col[:, 0:1], scalar2=None, op0=ALU.mult
+                )
+            else:
+                y_ps = vecs.tile([P, B], F32, tag="vec")
+                for c in range(CHUNKS):
+                    nc.tensor.matmul(
+                        out=y_ps[:],
+                        lhsT=g_cols[:, c, :],
+                        rhs=b_vec[:, r - 1, c, :],
+                        start=(c == 0),
+                        stop=(c == CHUNKS - 1),
+                    )
+                nc.vector.reciprocal(out=a_vec[:, r, :], in_=y_ps[:])
+                nc.vector.tensor_mul(out=a_vec[:, r, :], in0=a_vec[:, r, :], in1=own_image[:])
+            if r == ROUNDS - 1:
+                nc.vector.reduce_sum(out=a_col[:], in_=a_vec[:, r, :], axis=AXIS_X)
+                bcast_ps = vecs.tile([P, 2, BK], F32, tag="vec")
+                nc.tensor.matmul(
+                    out=bcast_ps[:, 0, :], lhsT=a_col[:, 0:1].to_broadcast([P, P]), rhs=ident[:], start=True, stop=True
+                )
+                nc.scalar.activation(out=ln_a[:], in_=a_col[:], func=ACT.Ln)
+                nc.scalar.activation(out=alpha_col[:], in_=ln_a[:], func=ACT.Exp, scale=inv_temp[:, 0:1])
+            z_ps = vecs.tile([P, CHUNKS, B], F32, tag="vec")
+            for c in range(CHUNKS):
+                nc.tensor.matmul(
+                    out=z_ps[:, c, :], lhsT=g_rows[:, c * P : (c + 1) * P], rhs=a_vec[:, r, :], start=True, stop=True
+                )
+            nc.vector.reciprocal(out=b_vec[:, r], in_=z_ps[:])
+
+        nc.tensor.matmul(
+            out=bcast_ps[:, 1, :], lhsT=alpha_col[:, 0:1].to_broadcast([P, P]), rhs=ident[:], start=True, stop=True
+        )
+        b_last = b_vec[:, ROUNDS - 1]
+        ln_b = keep.tile([P, CHUNKS, B], F32)
+        beta = keep.tile([P, CHUNKS, B], F32)
+        nc.scalar.activation(out=ln_b[:], in_=b_last, func=ACT.Ln)
+        nc.scalar.activation(out=beta[:], in_=ln_b[:], func=ACT.Exp, scale=inv_temp[:, 0:1])
+
+        ga = keep.tile([P, CHUNKS, BK], F32)
+        gta = keep.tile([P, CHUNKS, BK], F32)
+        nc.vector.tensor_tensor(
+            out=ga[:], in0=g_cols[:], in1=bcast_ps[:, 0, :].unsqueeze(1).to_broadcast([P, CHUNKS, BK]), op=ALU.mult
+        )
+        nc.vector.tensor_tensor(
+            out=gta[:], in0=gt_cols[:], in1=bcast_ps[:, 1, :].unsqueeze(1).to_broadcast([P, CHUNKS, BK]), op=ALU.mult
+        )
+        plain = keep.tile([P, CHUNKS, BK], F32)
+        tempered = keep.tile([P, CHUNKS, BK], F32)
+        nc.vector.tensor_tensor(
+            out=plain[:].rearrange("p c (b k) -> p c b k", b=B),
+            in0=ga[:].rearrange("p c (b k) -> p c b k", b=B),
+            in1=b_last.unsqueeze(3).to_broadcast([P, CHUNKS, B, K]),
+            op=ALU.mult,
+        )
+        nc.vector.tensor_tensor(
+            out=tempered[:].rearrange("p c (b k) -> p c b k", b=B),
+            in0=gta[:].rearrange("p c (b k) -> p c b k", b=B),
+            in1=beta[:].unsqueeze(3).to_broadcast([P, CHUNKS, B, K]),
+            op=ALU.mult,
+        )
+        p_grouped = keep.tile([P, PASSES, BK, PACK], BF16, align_bytes=64)
+        p_codes = keep.tile([P, PASSES, BK], U32, align_bytes=64)
+        p_scales = keep.tile([P, PASSES, BK], U8, align_bytes=64)
+        for g in range(PASSES):
+            chunks = slice(g * PACK, (g + 1) * PACK)
+            nc.vector.tensor_tensor(
+                out=p_grouped[:, g],
+                in0=plain[:, chunks, :].rearrange("p t m -> p m t"),
+                in1=tempered[:, chunks, :].rearrange("p t m -> p m t"),
+                op=ALU.add,
+            )
+        nc.vector.quantize_mx(
+            out=p_codes[:].rearrange("p g m -> p (g m)").bitcast(FP8X4),
+            scales=p_scales[:].rearrange("p g m -> p (g m)"),
+            in_=p_grouped[:].rearrange("p g m t -> p (g m t)"),
+        )
+
+        w_words = w_rows[:].bitcast(F32).rearrange("d (p u) -> d u p", u=2)
+        w_ps = lone.tile([P, 2, D], F32, tag="lone")
+        for u in range(2):
+            nc.tensor.transpose(w_ps[:, u, :], w_words[:, u, :], ident[:])
+        w_grouped = keep.tile([P, D * PACK], BF16, align_bytes=64)
+        nc.vector.tensor_copy(
+            out=w_grouped[:].bitcast(F32).rearrange("p (d u) -> p d u", u=2), in_=w_ps[:].rearrange("p u d -> p d u")
+        )
+        w_codes = keep.tile([P, D], U32, align_bytes=64)
+        w_scales = keep.tile([P, D], U8, align_bytes=64)
+        nc.vector.quantize_mx(out=w_codes[:].bitcast(FP8X4), scales=w_scales[:], in_=w_grouped[:])
+
+        h_grouped = keep.tile([P, B, N, PACK], BF16, align_bytes=64)
+        h_codes = keep.tile([P, B, N], U32, align_bytes=64)
+        h_scales = keep.tile([P, B, N], U8, align_bytes=64)
+        f_grouped = keep.tile([P, B, PASSES, D, PACK], BF16, align_bytes=64)
+        f_codes = keep.tile([P, B, PASSES, D], U32, align_bytes=64)
+        f_scales = keep.tile([P, B, PASSES, D], U8, align_bytes=64)
+        for b in range(B):
+            for g in range(PASSES):
+                pixels = slice(g * P * PACK, (g + 1) * P * PACK)
+                regroup_out = h_grouped[:, b, pixels, :].rearrange("p (c i) j -> p c j i", i=4)
+                regroup_in = h_raw[:, b, :, pixels].rearrange("p j (c i) -> p c j i", i=4)
+                if g == 0:
+                    nc.vector.tensor_copy(out=regroup_out, in_=regroup_in)
+                else:
+                    nc.scalar.copy(out=regroup_out, in_=regroup_in)
+            for g in range(PASSES):
+                pixels = slice(g * P * PACK, (g + 1) * P * PACK)
+                nc.vector.quantize_mx(
+                    out=h_codes[:, b, pixels].bitcast(FP8X4),
+                    scales=h_scales[:, b, pixels],
+                    in_=h_grouped[:, b, pixels, :].rearrange("p n j -> p (n j)"),
+                )
+        for b in range(B):
+            for g in range(PASSES):
+                f_ps = banks.tile([P, PACK, D], F32, tag="bank")
+                for t in range(PACK):
+                    cols = slice((g * PACK + t) * P, (g * PACK + t + 1) * P)
+                    nc.tensor.matmul_mx(
+                        out=f_ps[:, t, :],
+                        lhsT=h_codes[:, b, cols].bitcast(FP8X4),
+                        lhsT_scale=h_scales[:, b, cols],
+                        rhs=w_codes[:].bitcast(FP8X4),
+                        rhs_scale=w_scales[:],
+                        start=True,
+                        stop=True,
+                    )
+                nc.vector.tensor_tensor(
+                    out=f_grouped[:, b, g],
+                    in0=f_ps[:].rearrange("p t d -> p d t"),
+                    in1=bias_rows[:].unsqueeze(2).to_broadcast([P, D, PACK]),
+                    op=ALU.add,
+                )
+            nc.vector.quantize_mx(
+                out=f_codes[:, b].rearrange("p g d -> p (g d)").bitcast(FP8X4),
+                scales=f_scales[:, b].rearrange("p g d -> p (g d)"),
+                in_=f_grouped[:, b].rearrange("p g d t -> p (g d t)"),
+            )
+
+        agg_ps = lone.tile([P, B, BK], F32, tag="lone")
+        for b in range(B):
+            for g in range(PASSES):
+                nc.tensor.matmul_mx(
+                    out=agg_ps[:, b, :],
+                    lhsT=f_codes[:, b, g, :].bitcast(FP8X4),
+                    lhsT_scale=f_scales[:, b, g, :],
+                    rhs=p_codes[:, g, :].bitcast(FP8X4),
+                    rhs_scale=p_scales[:, g, :],
+                    start=(g == 0),
+                    stop=(g == PASSES - 1),
+                )
+
+        squares = keep.tile([P, B, K], F32)
+        square_sums = keep.tile([P, B], F32)
+        for b in range(B):
+            nc.scalar.activation(
+                out=squares[:, b, :],
+                in_=agg_ps[:, b, b * K : (b + 1) * K],
+                func=ACT.Square,
+                accum_out=square_sums[:, b : b + 1],
+            )
+        total_ps = vecs.tile([P, B], F32, tag="vec")
+        nc.tensor.matmul(out=total_ps[:], lhsT=ones[:], rhs=square_sums[:], start=True, stop=True)
+        norm = keep.tile([P, B], F32)
+        nc.vector.tensor_scalar_max(out=norm[:], in0=total_ps[:], scalar1=1e-24)
+        nc.scalar.activation(out=norm[:], in_=norm[:], func=ACT.Sqrt)
+        inv_norm = keep.tile([P, B], F32)
+        nc.vector.reciprocal(out=inv_norm[:], in_=norm[:])
+        result = keep.tile([P, B, K], F32)
+        for b in range(B):
+            nc.vector.tensor_scalar(
+                out=result[:, b, :],
+                in0=agg_ps[:, b, b * K : (b + 1) * K],
+                scalar1=inv_norm[:, b : b + 1],
+                scalar2=None,
+                op0=ALU.mult,
+            )
+        nc.sync.dma_start(out=out.rearrange("b (d k) -> d b k", k=K), in_=result[:])

@@ -19,6 +19,7 @@ BK = B * K
 CHUNKS = N // P
 PASSES = N // (P * PACK)
 ROUNDS = 3
+PIECES = B * PASSES
 
 FLOPS = 2 * B * (D * HID * N + D * K * N)
 
@@ -26,6 +27,7 @@ FLOPS = 2 * B * (D * HID * N + D * K * N)
 def tile_image_aggregation_pa_s_kernel(tc, h_cluster, w2c, b2c, scores, temperature, out):
     nc = tc.nc
     with ExitStack() as ctx:
+        ctx.enter_context(tc.manual_schedule())
         keep = ctx.enter_context(tc.tile_pool(name="keep", bufs=1))
         banks = ctx.enter_context(tc.psum_pool(name="banks", bufs=4))
         vecs = ctx.enter_context(tc.psum_pool(name="vecs", bufs=3))
@@ -33,12 +35,16 @@ def tile_image_aggregation_pa_s_kernel(tc, h_cluster, w2c, b2c, scores, temperat
 
         ident = keep.tile([P, P], F32)
         make_identity(nc, ident[:])
+        ident_bf = keep.tile([P, P], BF16)
+        make_identity(nc, ident_bf[:])
         ones = keep.tile([P, P], F32)
         nc.gpsimd.memset(ones[:], 1.0)
         own_image = keep.tile([P, B], F32)
         nc.vector.memset(own_image[:], 0.0)
         for b in range(B):
             nc.vector.memset(own_image[b * K : (b + 1) * K, b : b + 1], 1.0)
+        minus_half = keep.tile([P, B], F32)
+        nc.vector.memset(minus_half[:], -0.5)
 
         s_rows = keep.tile([P, N], BF16)
         nc.sync.dma_start(out=s_rows[:], in_=scores.rearrange("b k n -> (b k) n"))
@@ -52,8 +58,64 @@ def tile_image_aggregation_pa_s_kernel(tc, h_cluster, w2c, b2c, scores, temperat
         for b in range(B):
             nc.sync.dma_start(out=h_raw[:, b], in_=h_cluster[b].rearrange("(p j) n -> p j n", j=PACK))
 
-        inv_temp = keep.tile([P, 1], F32)
-        nc.vector.reciprocal(out=inv_temp[:], in_=temp[:])
+        w_grouped = keep.tile([P, D * PACK], BF16, align_bytes=64)
+        w_codes = keep.tile([P, D], U32, align_bytes=64)
+        w_scales = keep.tile([P, D], U8, align_bytes=64)
+        h_grouped = keep.tile([P, B, N, PACK], BF16, align_bytes=64)
+        h_codes = keep.tile([P, B, N], U32, align_bytes=64)
+        h_scales = keep.tile([P, B, N], U8, align_bytes=64)
+        f_grouped = keep.tile([P, B, PASSES, D, PACK], BF16, align_bytes=64)
+        f_codes = keep.tile([P, B, PASSES, D], U32, align_bytes=64)
+        f_scales = keep.tile([P, B, PASSES, D], U8, align_bytes=64)
+        f_ps = {}
+
+        def regroup_h(q, copy):
+            b, g = q % B, q // B
+            pixels = slice(g * P * PACK, (g + 1) * P * PACK)
+            copy(
+                out=h_grouped[:, b, pixels, :].rearrange("p (c i) j -> p c j i", i=4),
+                in_=h_raw[:, b, :, pixels].rearrange("p j (c i) -> p c j i", i=4),
+            )
+
+        def quantise_h(q):
+            b, g = q % B, q // B
+            pixels = slice(g * P * PACK, (g + 1) * P * PACK)
+            nc.vector.quantize_mx(
+                out=h_codes[:, b, pixels].bitcast(FP8X4),
+                scales=h_scales[:, b, pixels],
+                in_=h_grouped[:, b, pixels, :].rearrange("p n j -> p (n j)"),
+            )
+
+        def multiply_f(q):
+            b, g = q % B, q // B
+            f_ps[q] = banks.tile([P, PACK, D], F32, tag="bank", name="f_ps%d" % q)
+            for t in range(PACK):
+                cols = slice((g * PACK + t) * P, (g * PACK + t + 1) * P)
+                nc.tensor.matmul_mx(
+                    out=f_ps[q][:, t, :],
+                    lhsT=h_codes[:, b, cols].bitcast(FP8X4),
+                    lhsT_scale=h_scales[:, b, cols],
+                    rhs=w_codes[:].bitcast(FP8X4),
+                    rhs_scale=w_scales[:],
+                    start=True,
+                    stop=True,
+                )
+
+        def add_bias(q):
+            b, g = q % B, q // B
+            nc.vector.tensor_tensor(
+                out=f_grouped[:, b, g],
+                in0=f_ps[q][:].rearrange("p t d -> p d t"),
+                in1=bias_rows[:].unsqueeze(2).to_broadcast([P, D, PACK]),
+                op=ALU.add,
+            )
+
+        def quantise_f(b):
+            nc.vector.quantize_mx(
+                out=f_codes[:, b].rearrange("p g d -> p (g d)").bitcast(FP8X4),
+                scales=f_scales[:, b].rearrange("p g d -> p (g d)"),
+                in_=f_grouped[:, b].rearrange("p g d t -> p (g d t)"),
+            )
 
         rowmax = keep.tile([P, 1], F32)
         nc.vector.reduce_max(out=rowmax[:], in_=s_rows[:], axis=AXIS_X)
@@ -62,18 +124,31 @@ def tile_image_aggregation_pa_s_kernel(tc, h_cluster, w2c, b2c, scores, temperat
         dm_cols = keep.tile([P, CHUNKS, BK], F32)
         g_cols = keep.tile([P, CHUNKS, BK], F32)
         gt_cols = keep.tile([P, CHUNKS, BK], F32)
-        g_rows = keep.tile([P, N], F32)
+        g_cols_pair = keep.tile([P, 2, CHUNKS, BK], BF16)
+        g_rows_pair = keep.tile([P, 2, N], BF16)
+        d_cols_ps = {}
         for g in range(PASSES):
             pixels = slice(g * P * PACK, (g + 1) * P * PACK)
-            chunks = slice(g * PACK, (g + 1) * PACK)
             nc.vector.tensor_scalar(
                 out=d_rows[:, pixels], in0=s_rows[:, pixels], scalar1=rowmax[:, 0:1], scalar2=None, op0=ALU.subtract
             )
-            d_cols_ps = banks.tile([P, PACK, BK], F32, tag="bank")
+            d_cols_ps[g] = banks.tile([P, PACK, BK], F32, tag="bank", name="d_cols_ps%d" % g)
             for t in range(PACK):
                 c = g * PACK + t
-                nc.tensor.transpose(d_cols_ps[:, t, :], d_rows[:, c * P : (c + 1) * P], ident[:])
-            by_image = d_cols_ps[:].rearrange("p t (b k) -> p t b k", b=B)
+                nc.tensor.transpose(d_cols_ps[g][:, t, :], d_rows[:, c * P : (c + 1) * P], ident[:])
+
+        unused = keep.tile([P, N], BF16)
+        rowsum = keep.tile([P, 1], F32)
+        nc.scalar.activation(out=unused[:], in_=d_rows[:], func=ACT.Exp, accum_out=rowsum[:])
+
+        w_words = w_rows[:].bitcast(F32).rearrange("d (p u) -> d u p", u=2)
+        w_ps = lone.tile([P, 2, D], F32, tag="lone")
+        for u in range(2):
+            nc.tensor.transpose(w_ps[:, u, :], w_words[:, u, :], ident[:])
+
+        for g in range(PASSES):
+            chunks = slice(g * PACK, (g + 1) * PACK)
+            by_image = d_cols_ps[g][:].rearrange("p t (b k) -> p t b k", b=B)
             nc.vector.tensor_reduce(out=colmax[:, chunks, :], in_=by_image, axis=AXIS_X, op=ALU.max)
             nc.vector.tensor_tensor(
                 out=dm_cols[:, chunks, :].rearrange("p t (b k) -> p t b k", b=B),
@@ -82,175 +157,172 @@ def tile_image_aggregation_pa_s_kernel(tc, h_cluster, w2c, b2c, scores, temperat
                 op=ALU.subtract,
             )
             nc.scalar.activation(out=g_cols[:, chunks, :], in_=dm_cols[:, chunks, :], func=ACT.Exp)
-
-        unused = keep.tile([P, N], BF16)
-        rowsum = keep.tile([P, 1], F32)
-        nc.scalar.activation(out=unused[:], in_=d_rows[:], func=ACT.Exp, accum_out=rowsum[:])
-
+            nc.scalar.activation(out=g_cols_pair[:, 0, chunks, :], in_=dm_cols[:, chunks, :], func=ACT.Exp)
         for g in range(PASSES):
             pixels = slice(g * P * PACK, (g + 1) * P * PACK)
-            g_rows_ps = banks.tile([P, PACK, P], F32, tag="bank")
-            for t in range(PACK):
-                nc.tensor.transpose(g_rows_ps[:, t, :], g_cols[:, g * PACK + t, :], ident[:])
-            if g == 0:
-                nc.vector.tensor_copy(out=g_rows[:, pixels], in_=g_rows_ps[:].rearrange("p t n -> p (t n)"))
-            else:
-                nc.scalar.copy(out=g_rows[:, pixels], in_=g_rows_ps[:].rearrange("p t n -> p (t n)"))
+            chunks = slice(g * PACK, (g + 1) * PACK)
+            nc.vector.tensor_tensor(
+                out=g_cols_pair[:, 1, chunks, :],
+                in0=g_cols[:, chunks, :],
+                in1=g_cols_pair[:, 0, chunks, :],
+                op=ALU.subtract,
+            )
+            pair_ps = banks.tile([P, 2, PACK, P], BF16, tag="bank")
+            for i in range(2):
+                for t in range(PACK):
+                    nc.tensor.transpose(pair_ps[:, i, t, :], g_cols_pair[:, i, g * PACK + t, :], ident_bf[:])
+            nc.scalar.copy(out=g_rows_pair[:, :, pixels], in_=pair_ps[:].rearrange("p i t n -> p i (t n)"))
 
+        a_own = keep.tile([P, B], F32)
+        a_pair = keep.tile([P, 2, B], BF16)
+        inv_sum = keep.tile([P, B], F32)
+        nc.vector.reciprocal(out=inv_sum[:, 0:1], in_=rowsum[:])
+        nc.vector.tensor_scalar(out=a_own[:], in0=own_image[:], scalar1=inv_sum[:, 0:1], scalar2=None, op0=ALU.mult)
+        nc.vector.tensor_copy(out=a_pair[:, 0, :], in_=a_own[:])
+        nc.vector.tensor_tensor(out=a_pair[:, 1, :], in0=a_own[:], in1=a_pair[:, 0, :], op=ALU.subtract)
+
+        inv_temp = keep.tile([P, 1], F32)
+        nc.vector.reciprocal(out=inv_temp[:], in_=temp[:])
+        neg_inv_temp = keep.tile([P, 1], F32)
+        nc.vector.tensor_scalar_mul(out=neg_inv_temp[:], in0=inv_temp[:], scalar1=-1.0)
+        nc.vector.tensor_copy(
+            out=w_grouped[:].bitcast(F32).rearrange("p (d u) -> p d u", u=2), in_=w_ps[:].rearrange("p u d -> p d u")
+        )
+        regroup_h(0, nc.vector.tensor_copy)
+        nc.vector.quantize_mx(out=w_codes[:].bitcast(FP8X4), scales=w_scales[:], in_=w_grouped[:])
+        regroup_h(1, nc.vector.tensor_copy)
+        quantise_h(0)
+        regroup_h(2, nc.scalar.copy)
+        regroup_h(3, nc.scalar.copy)
         nc.scalar.activation(out=gt_cols[:], in_=dm_cols[:], func=ACT.Exp, scale=inv_temp[:, 0:1])
 
-        a_vec = keep.tile([P, ROUNDS, B], F32)
-        b_vec = keep.tile([P, ROUNDS, CHUNKS, B], F32)
-        bcast_ps = None
+        def ride_along_tensor(s):
+            if s < PIECES:
+                multiply_f(s)
+
+        def ride_along_vector(s):
+            if s + 1 < PIECES:
+                quantise_h(s + 1)
+            if s < PIECES:
+                add_bias(s)
+
+        z_sum = keep.tile([P, CHUNKS, B], F32)
+        b_vec = keep.tile([P, CHUNKS, B], F32)
+        b_pair = keep.tile([P, CHUNKS, 2, B], BF16)
         a_col = keep.tile([P, 1], F32)
-        ln_a = keep.tile([P, 1], F32)
         alpha_col = keep.tile([P, 1], F32)
+        ga = keep.tile([P, CHUNKS, BK], F32)
+        a_rows_ps = None
+        alpha_rows_ps = None
         for r in range(ROUNDS):
-            if r == 0:
-                nc.vector.reciprocal(out=a_col[:], in_=rowsum[:])
-                nc.vector.tensor_scalar(
-                    out=a_vec[:, r, :], in0=own_image[:], scalar1=a_col[:, 0:1], scalar2=None, op0=ALU.mult
-                )
-            else:
-                y_ps = vecs.tile([P, B], F32, tag="vec")
-                for c in range(CHUNKS):
-                    nc.tensor.matmul(
-                        out=y_ps[:],
-                        lhsT=g_cols[:, c, :],
-                        rhs=b_vec[:, r - 1, c, :],
-                        start=(c == 0),
-                        stop=(c == CHUNKS - 1),
-                    )
-                nc.vector.reciprocal(out=a_vec[:, r, :], in_=y_ps[:])
-                nc.vector.tensor_mul(out=a_vec[:, r, :], in0=a_vec[:, r, :], in1=own_image[:])
-            if r == ROUNDS - 1:
-                nc.vector.reduce_sum(out=a_col[:], in_=a_vec[:, r, :], axis=AXIS_X)
-                bcast_ps = vecs.tile([P, 2, BK], F32, tag="vec")
-                nc.tensor.matmul(
-                    out=bcast_ps[:, 0, :], lhsT=a_col[:, 0:1].to_broadcast([P, P]), rhs=ident[:], start=True, stop=True
-                )
-                nc.scalar.activation(out=ln_a[:], in_=a_col[:], func=ACT.Ln)
-                nc.scalar.activation(out=alpha_col[:], in_=ln_a[:], func=ACT.Exp, scale=inv_temp[:, 0:1])
-            z_ps = vecs.tile([P, CHUNKS, B], F32, tag="vec")
+            last = r == ROUNDS - 1
+            if last:
+                a_rows_ps = vecs.tile([P, BK], F32, tag="vec")
+                nc.tensor.transpose(a_rows_ps[:], a_col[:, 0:1].to_broadcast([P, P]), ident[:])
+            z_ps = vecs.tile([P, CHUNKS, 2, B], F32, tag="vec")
             for c in range(CHUNKS):
                 nc.tensor.matmul(
-                    out=z_ps[:, c, :], lhsT=g_rows[:, c * P : (c + 1) * P], rhs=a_vec[:, r, :], start=True, stop=True
+                    out=z_ps[:, c].rearrange("p i b -> p (i b)"),
+                    lhsT=g_rows_pair[:, 0, c * P : (c + 1) * P],
+                    rhs=a_pair[:].rearrange("p i b -> p (i b)"),
+                    start=True,
+                    stop=False,
                 )
-            nc.vector.reciprocal(out=b_vec[:, r], in_=z_ps[:])
+                nc.tensor.matmul(
+                    out=z_ps[:, c, 0, :],
+                    lhsT=g_rows_pair[:, 1, c * P : (c + 1) * P],
+                    rhs=a_pair[:, 0, :],
+                    start=False,
+                    stop=True,
+                )
+            ride_along_tensor(2 * r)
+            if last:
+                alpha_rows_ps = vecs.tile([P, BK], F32, tag="vec")
+                nc.tensor.transpose(alpha_rows_ps[:], alpha_col[:, 0:1].to_broadcast([P, P]), ident[:])
+                nc.vector.tensor_tensor(
+                    out=ga[:], in0=g_cols[:], in1=a_rows_ps[:].unsqueeze(1).to_broadcast([P, CHUNKS, BK]), op=ALU.mult
+                )
+            nc.vector.tensor_reduce(out=z_sum[:], in_=z_ps[:].rearrange("p c i b -> p c b i"), axis=AXIS_X, op=ALU.add)
+            nc.vector.reciprocal(out=b_vec[:], in_=z_sum[:])
+            if last:
+                break
+            nc.vector.tensor_copy(out=b_pair[:, :, 0, :], in_=b_vec[:])
+            nc.vector.tensor_tensor(out=b_pair[:, :, 1, :], in0=b_vec[:], in1=b_pair[:, :, 0, :], op=ALU.subtract)
+            ride_along_vector(2 * r)
 
-        nc.tensor.matmul(
-            out=bcast_ps[:, 1, :], lhsT=alpha_col[:, 0:1].to_broadcast([P, P]), rhs=ident[:], start=True, stop=True
-        )
-        b_last = b_vec[:, ROUNDS - 1]
-        ln_b = keep.tile([P, CHUNKS, B], F32)
+            y_ps = vecs.tile([P, 2, B], F32, tag="vec")
+            for c in range(CHUNKS):
+                nc.tensor.matmul(
+                    out=y_ps[:].rearrange("p i b -> p (i b)"),
+                    lhsT=g_cols_pair[:, 0, c, :],
+                    rhs=b_pair[:, c].rearrange("p i b -> p (i b)"),
+                    start=(c == 0),
+                    stop=False,
+                )
+                nc.tensor.matmul(
+                    out=y_ps[:, 0, :],
+                    lhsT=g_cols_pair[:, 1, c, :],
+                    rhs=b_pair[:, c, 0, :],
+                    start=False,
+                    stop=(c == CHUNKS - 1),
+                )
+            ride_along_tensor(2 * r + 1)
+            nc.vector.tensor_reduce(out=inv_sum[:], in_=y_ps[:].rearrange("p i b -> p b i"), axis=AXIS_X, op=ALU.add)
+            nc.vector.reciprocal(out=inv_sum[:], in_=inv_sum[:])
+            nc.vector.tensor_mul(out=a_own[:], in0=inv_sum[:], in1=own_image[:])
+            if r == ROUNDS - 2:
+                nc.vector.reduce_sum(out=a_col[:], in_=a_own[:], axis=AXIS_X)
+                nc.gpsimd.tensor_tensor(out=alpha_col[:], in0=a_col[:], in1=inv_temp[:], op=ALU.pow)
+            nc.vector.tensor_copy(out=a_pair[:, 0, :], in_=a_own[:])
+            nc.vector.tensor_tensor(out=a_pair[:, 1, :], in0=a_own[:], in1=a_pair[:, 0, :], op=ALU.subtract)
+            ride_along_vector(2 * r + 1)
+
+        ln_z = keep.tile([P, CHUNKS, B], F32)
         beta = keep.tile([P, CHUNKS, B], F32)
-        nc.scalar.activation(out=ln_b[:], in_=b_last, func=ACT.Ln)
-        nc.scalar.activation(out=beta[:], in_=ln_b[:], func=ACT.Exp, scale=inv_temp[:, 0:1])
-
-        ga = keep.tile([P, CHUNKS, BK], F32)
+        nc.scalar.activation(out=ln_z[:], in_=z_sum[:], func=ACT.Ln)
+        nc.scalar.activation(out=beta[:], in_=ln_z[:], func=ACT.Exp, scale=neg_inv_temp[:, 0:1])
         gta = keep.tile([P, CHUNKS, BK], F32)
-        nc.vector.tensor_tensor(
-            out=ga[:], in0=g_cols[:], in1=bcast_ps[:, 0, :].unsqueeze(1).to_broadcast([P, CHUNKS, BK]), op=ALU.mult
-        )
-        nc.vector.tensor_tensor(
-            out=gta[:], in0=gt_cols[:], in1=bcast_ps[:, 1, :].unsqueeze(1).to_broadcast([P, CHUNKS, BK]), op=ALU.mult
-        )
         plain = keep.tile([P, CHUNKS, BK], F32)
         tempered = keep.tile([P, CHUNKS, BK], F32)
         nc.vector.tensor_tensor(
             out=plain[:].rearrange("p c (b k) -> p c b k", b=B),
             in0=ga[:].rearrange("p c (b k) -> p c b k", b=B),
-            in1=b_last.unsqueeze(3).to_broadcast([P, CHUNKS, B, K]),
+            in1=b_vec[:].unsqueeze(3).to_broadcast([P, CHUNKS, B, K]),
             op=ALU.mult,
         )
         nc.vector.tensor_tensor(
-            out=tempered[:].rearrange("p c (b k) -> p c b k", b=B),
-            in0=gta[:].rearrange("p c (b k) -> p c b k", b=B),
-            in1=beta[:].unsqueeze(3).to_broadcast([P, CHUNKS, B, K]),
-            op=ALU.mult,
+            out=gta[:], in0=gt_cols[:], in1=alpha_rows_ps[:].unsqueeze(1).to_broadcast([P, CHUNKS, BK]), op=ALU.mult
         )
+        for b in range(B):
+            quantise_f(b)
         p_grouped = keep.tile([P, PASSES, BK, PACK], BF16, align_bytes=64)
         p_codes = keep.tile([P, PASSES, BK], U32, align_bytes=64)
         p_scales = keep.tile([P, PASSES, BK], U8, align_bytes=64)
+        agg_ps = {}
+        for b in range(B):
+            agg_ps[b] = banks.tile([P, BK], F32, tag="bank", name="agg_ps%d" % b)
         for g in range(PASSES):
             chunks = slice(g * PACK, (g + 1) * PACK)
+            nc.vector.tensor_tensor(
+                out=tempered[:, chunks, :].rearrange("p c (b k) -> p c b k", b=B),
+                in0=gta[:, chunks, :].rearrange("p c (b k) -> p c b k", b=B),
+                in1=beta[:, chunks, :].unsqueeze(3).to_broadcast([P, PACK, B, K]),
+                op=ALU.mult,
+            )
             nc.vector.tensor_tensor(
                 out=p_grouped[:, g],
                 in0=plain[:, chunks, :].rearrange("p t m -> p m t"),
                 in1=tempered[:, chunks, :].rearrange("p t m -> p m t"),
                 op=ALU.add,
             )
-        nc.vector.quantize_mx(
-            out=p_codes[:].rearrange("p g m -> p (g m)").bitcast(FP8X4),
-            scales=p_scales[:].rearrange("p g m -> p (g m)"),
-            in_=p_grouped[:].rearrange("p g m t -> p (g m t)"),
-        )
-
-        w_words = w_rows[:].bitcast(F32).rearrange("d (p u) -> d u p", u=2)
-        w_ps = lone.tile([P, 2, D], F32, tag="lone")
-        for u in range(2):
-            nc.tensor.transpose(w_ps[:, u, :], w_words[:, u, :], ident[:])
-        w_grouped = keep.tile([P, D * PACK], BF16, align_bytes=64)
-        nc.vector.tensor_copy(
-            out=w_grouped[:].bitcast(F32).rearrange("p (d u) -> p d u", u=2), in_=w_ps[:].rearrange("p u d -> p d u")
-        )
-        w_codes = keep.tile([P, D], U32, align_bytes=64)
-        w_scales = keep.tile([P, D], U8, align_bytes=64)
-        nc.vector.quantize_mx(out=w_codes[:].bitcast(FP8X4), scales=w_scales[:], in_=w_grouped[:])
-
-        h_grouped = keep.tile([P, B, N, PACK], BF16, align_bytes=64)
-        h_codes = keep.tile([P, B, N], U32, align_bytes=64)
-        h_scales = keep.tile([P, B, N], U8, align_bytes=64)
-        f_grouped = keep.tile([P, B, PASSES, D, PACK], BF16, align_bytes=64)
-        f_codes = keep.tile([P, B, PASSES, D], U32, align_bytes=64)
-        f_scales = keep.tile([P, B, PASSES, D], U8, align_bytes=64)
-        for b in range(B):
-            for g in range(PASSES):
-                pixels = slice(g * P * PACK, (g + 1) * P * PACK)
-                regroup_out = h_grouped[:, b, pixels, :].rearrange("p (c i) j -> p c j i", i=4)
-                regroup_in = h_raw[:, b, :, pixels].rearrange("p j (c i) -> p c j i", i=4)
-                if g == 0:
-                    nc.vector.tensor_copy(out=regroup_out, in_=regroup_in)
-                else:
-                    nc.scalar.copy(out=regroup_out, in_=regroup_in)
-            for g in range(PASSES):
-                pixels = slice(g * P * PACK, (g + 1) * P * PACK)
-                nc.vector.quantize_mx(
-                    out=h_codes[:, b, pixels].bitcast(FP8X4),
-                    scales=h_scales[:, b, pixels],
-                    in_=h_grouped[:, b, pixels, :].rearrange("p n j -> p (n j)"),
-                )
-        for b in range(B):
-            for g in range(PASSES):
-                f_ps = banks.tile([P, PACK, D], F32, tag="bank")
-                for t in range(PACK):
-                    cols = slice((g * PACK + t) * P, (g * PACK + t + 1) * P)
-                    nc.tensor.matmul_mx(
-                        out=f_ps[:, t, :],
-                        lhsT=h_codes[:, b, cols].bitcast(FP8X4),
-                        lhsT_scale=h_scales[:, b, cols],
-                        rhs=w_codes[:].bitcast(FP8X4),
-                        rhs_scale=w_scales[:],
-                        start=True,
-                        stop=True,
-                    )
-                nc.vector.tensor_tensor(
-                    out=f_grouped[:, b, g],
-                    in0=f_ps[:].rearrange("p t d -> p d t"),
-                    in1=bias_rows[:].unsqueeze(2).to_broadcast([P, D, PACK]),
-                    op=ALU.add,
-                )
             nc.vector.quantize_mx(
-                out=f_codes[:, b].rearrange("p g d -> p (g d)").bitcast(FP8X4),
-                scales=f_scales[:, b].rearrange("p g d -> p (g d)"),
-                in_=f_grouped[:, b].rearrange("p g d t -> p (g d t)"),
+                out=p_codes[:, g, :].bitcast(FP8X4),
+                scales=p_scales[:, g, :],
+                in_=p_grouped[:, g].rearrange("p m t -> p (m t)"),
             )
-
-        agg_ps = lone.tile([P, B, BK], F32, tag="lone")
-        for b in range(B):
-            for g in range(PASSES):
+            for b in range(B):
                 nc.tensor.matmul_mx(
-                    out=agg_ps[:, b, :],
+                    out=agg_ps[b][:],
                     lhsT=f_codes[:, b, g, :].bitcast(FP8X4),
                     lhsT_scale=f_scales[:, b, g, :],
                     rhs=p_codes[:, g, :].bitcast(FP8X4),
@@ -264,22 +336,21 @@ def tile_image_aggregation_pa_s_kernel(tc, h_cluster, w2c, b2c, scores, temperat
         for b in range(B):
             nc.scalar.activation(
                 out=squares[:, b, :],
-                in_=agg_ps[:, b, b * K : (b + 1) * K],
+                in_=agg_ps[b][:, b * K : (b + 1) * K],
                 func=ACT.Square,
                 accum_out=square_sums[:, b : b + 1],
             )
         total_ps = vecs.tile([P, B], F32, tag="vec")
         nc.tensor.matmul(out=total_ps[:], lhsT=ones[:], rhs=square_sums[:], start=True, stop=True)
-        norm = keep.tile([P, B], F32)
-        nc.vector.tensor_scalar_max(out=norm[:], in0=total_ps[:], scalar1=1e-24)
-        nc.scalar.activation(out=norm[:], in_=norm[:], func=ACT.Sqrt)
+        clamped = keep.tile([P, B], F32)
+        nc.vector.tensor_scalar_max(out=clamped[:], in0=total_ps[:], scalar1=1e-24)
         inv_norm = keep.tile([P, B], F32)
-        nc.vector.reciprocal(out=inv_norm[:], in_=norm[:])
+        nc.gpsimd.tensor_tensor(out=inv_norm[:], in0=clamped[:], in1=minus_half[:], op=ALU.pow)
         result = keep.tile([P, B, K], F32)
         for b in range(B):
             nc.vector.tensor_scalar(
                 out=result[:, b, :],
-                in0=agg_ps[:, b, b * K : (b + 1) * K],
+                in0=agg_ps[b][:, b * K : (b + 1) * K],
                 scalar1=inv_norm[:, b : b + 1],
                 scalar2=None,
                 op0=ALU.mult,

@@ -18,10 +18,28 @@ B, HID, N, D, K = 2, 512, 1024, 128, 64
 BK = B * K
 CHUNKS = N // P
 PASSES = N // (P * PACK)
-ROUNDS = 3
 PIECES = B * PASSES
+ROUNDS = 3
+HI, LO = 0, 1
+RUN = 4
 
 FLOPS = 2 * B * (D * HID * N + D * K * N)
+
+
+def pass_pixels(g):
+    return slice(g * P * PACK, (g + 1) * P * PACK)
+
+
+def pass_chunks(g):
+    return slice(g * PACK, (g + 1) * PACK)
+
+
+def chunk_pixels(c):
+    return slice(c * P, (c + 1) * P)
+
+
+def by_image(cols):
+    return cols.rearrange("p c (b k) -> p c b k", b=B)
 
 
 def tile_image_aggregation_pa_s_kernel(tc, h_cluster, w2c, b2c, scores, temperature, out):
@@ -71,30 +89,27 @@ def tile_image_aggregation_pa_s_kernel(tc, h_cluster, w2c, b2c, scores, temperat
 
         def regroup_h(q, copy):
             b, g = q % B, q // B
-            pixels = slice(g * P * PACK, (g + 1) * P * PACK)
             copy(
-                out=h_grouped[:, b, pixels, :].rearrange("p (c i) j -> p c j i", i=4),
-                in_=h_raw[:, b, :, pixels].rearrange("p j (c i) -> p c j i", i=4),
+                out=h_grouped[:, b, pass_pixels(g), :].rearrange("p (c i) j -> p c j i", i=RUN),
+                in_=h_raw[:, b, :, pass_pixels(g)].rearrange("p j (c i) -> p c j i", i=RUN),
             )
 
         def quantise_h(q):
             b, g = q % B, q // B
-            pixels = slice(g * P * PACK, (g + 1) * P * PACK)
             nc.vector.quantize_mx(
-                out=h_codes[:, b, pixels].bitcast(FP8X4),
-                scales=h_scales[:, b, pixels],
-                in_=h_grouped[:, b, pixels, :].rearrange("p n j -> p (n j)"),
+                out=h_codes[:, b, pass_pixels(g)].bitcast(FP8X4),
+                scales=h_scales[:, b, pass_pixels(g)],
+                in_=h_grouped[:, b, pass_pixels(g), :].rearrange("p n j -> p (n j)"),
             )
 
         def multiply_f(q):
             b, g = q % B, q // B
             f_ps[q] = banks.tile([P, PACK, D], F32, tag="bank", name="f_ps%d" % q)
             for t in range(PACK):
-                cols = slice((g * PACK + t) * P, (g * PACK + t + 1) * P)
                 nc.tensor.matmul_mx(
                     out=f_ps[q][:, t, :],
-                    lhsT=h_codes[:, b, cols].bitcast(FP8X4),
-                    lhsT_scale=h_scales[:, b, cols],
+                    lhsT=h_codes[:, b, chunk_pixels(g * PACK + t)].bitcast(FP8X4),
+                    lhsT_scale=h_scales[:, b, chunk_pixels(g * PACK + t)],
                     rhs=w_codes[:].bitcast(FP8X4),
                     rhs_scale=w_scales[:],
                     start=True,
@@ -120,66 +135,68 @@ def tile_image_aggregation_pa_s_kernel(tc, h_cluster, w2c, b2c, scores, temperat
         rowmax = keep.tile([P, 1], F32)
         nc.vector.reduce_max(out=rowmax[:], in_=s_rows[:], axis=AXIS_X)
         d_rows = keep.tile([P, N], F32)
-        colmax = keep.tile([P, CHUNKS, B], F32)
-        dm_cols = keep.tile([P, CHUNKS, BK], F32)
-        g_cols = keep.tile([P, CHUNKS, BK], F32)
-        gt_cols = keep.tile([P, CHUNKS, BK], F32)
-        g_cols_pair = keep.tile([P, 2, CHUNKS, BK], BF16)
-        g_rows_pair = keep.tile([P, 2, N], BF16)
         d_cols_ps = {}
         for g in range(PASSES):
-            pixels = slice(g * P * PACK, (g + 1) * P * PACK)
             nc.vector.tensor_scalar(
-                out=d_rows[:, pixels], in0=s_rows[:, pixels], scalar1=rowmax[:, 0:1], scalar2=None, op0=ALU.subtract
+                out=d_rows[:, pass_pixels(g)],
+                in0=s_rows[:, pass_pixels(g)],
+                scalar1=rowmax[:, 0:1],
+                scalar2=None,
+                op0=ALU.subtract,
             )
             d_cols_ps[g] = banks.tile([P, PACK, BK], F32, tag="bank", name="d_cols_ps%d" % g)
             for t in range(PACK):
-                c = g * PACK + t
-                nc.tensor.transpose(d_cols_ps[g][:, t, :], d_rows[:, c * P : (c + 1) * P], ident[:])
+                nc.tensor.transpose(d_cols_ps[g][:, t, :], d_rows[:, chunk_pixels(g * PACK + t)], ident[:])
 
-        unused = keep.tile([P, N], BF16)
-        rowsum = keep.tile([P, 1], F32)
-        nc.scalar.activation(out=unused[:], in_=d_rows[:], func=ACT.Exp, accum_out=rowsum[:])
+        exp_rows = keep.tile([P, N], BF16)
+        first_sum = keep.tile([P, 1], F32)
+        nc.scalar.activation(out=exp_rows[:], in_=d_rows[:], func=ACT.Exp, accum_out=first_sum[:])
 
         w_words = w_rows[:].bitcast(F32).rearrange("d (p u) -> d u p", u=2)
-        w_ps = lone.tile([P, 2, D], F32, tag="lone")
+        w_ps = lone.tile([P, 2, D], F32)
         for u in range(2):
             nc.tensor.transpose(w_ps[:, u, :], w_words[:, u, :], ident[:])
 
+        colmax = keep.tile([P, CHUNKS, B], F32)
+        dm_cols = keep.tile([P, CHUNKS, BK], F32)
+        g_cols = keep.tile([P, CHUNKS, BK], F32)
+        g_cols_pair = keep.tile([P, 2, CHUNKS, BK], BF16)
+        g_rows_pair = keep.tile([P, 2, N], BF16)
         for g in range(PASSES):
-            chunks = slice(g * PACK, (g + 1) * PACK)
-            by_image = d_cols_ps[g][:].rearrange("p t (b k) -> p t b k", b=B)
-            nc.vector.tensor_reduce(out=colmax[:, chunks, :], in_=by_image, axis=AXIS_X, op=ALU.max)
+            chunks = pass_chunks(g)
+            nc.vector.tensor_reduce(out=colmax[:, chunks, :], in_=by_image(d_cols_ps[g][:]), axis=AXIS_X, op=ALU.max)
             nc.vector.tensor_tensor(
-                out=dm_cols[:, chunks, :].rearrange("p t (b k) -> p t b k", b=B),
-                in0=by_image,
+                out=by_image(dm_cols[:, chunks, :]),
+                in0=by_image(d_cols_ps[g][:]),
                 in1=colmax[:, chunks, :].unsqueeze(3).to_broadcast([P, PACK, B, K]),
                 op=ALU.subtract,
             )
             nc.scalar.activation(out=g_cols[:, chunks, :], in_=dm_cols[:, chunks, :], func=ACT.Exp)
-            nc.scalar.activation(out=g_cols_pair[:, 0, chunks, :], in_=dm_cols[:, chunks, :], func=ACT.Exp)
+            nc.scalar.activation(out=g_cols_pair[:, HI, chunks, :], in_=dm_cols[:, chunks, :], func=ACT.Exp)
         for g in range(PASSES):
-            pixels = slice(g * P * PACK, (g + 1) * P * PACK)
-            chunks = slice(g * PACK, (g + 1) * PACK)
+            chunks = pass_chunks(g)
             nc.vector.tensor_tensor(
-                out=g_cols_pair[:, 1, chunks, :],
+                out=g_cols_pair[:, LO, chunks, :],
                 in0=g_cols[:, chunks, :],
-                in1=g_cols_pair[:, 0, chunks, :],
+                in1=g_cols_pair[:, HI, chunks, :],
                 op=ALU.subtract,
             )
             pair_ps = banks.tile([P, 2, PACK, P], BF16, tag="bank")
-            for i in range(2):
+            for part in (HI, LO):
                 for t in range(PACK):
-                    nc.tensor.transpose(pair_ps[:, i, t, :], g_cols_pair[:, i, g * PACK + t, :], ident_bf[:])
-            nc.scalar.copy(out=g_rows_pair[:, :, pixels], in_=pair_ps[:].rearrange("p i t n -> p i (t n)"))
+                    nc.tensor.transpose(pair_ps[:, part, t, :], g_cols_pair[:, part, g * PACK + t, :], ident_bf[:])
+            nc.scalar.copy(out=g_rows_pair[:, :, pass_pixels(g)], in_=pair_ps[:].rearrange("p i t n -> p i (t n)"))
 
+        def split(hi, lo, value):
+            nc.vector.tensor_copy(out=hi, in_=value)
+            nc.vector.tensor_tensor(out=lo, in0=value, in1=hi, op=ALU.subtract)
+
+        a_col = keep.tile([P, 1], F32)
         a_own = keep.tile([P, B], F32)
         a_pair = keep.tile([P, 2, B], BF16)
-        inv_sum = keep.tile([P, B], F32)
-        nc.vector.reciprocal(out=inv_sum[:, 0:1], in_=rowsum[:])
-        nc.vector.tensor_scalar(out=a_own[:], in0=own_image[:], scalar1=inv_sum[:, 0:1], scalar2=None, op0=ALU.mult)
-        nc.vector.tensor_copy(out=a_pair[:, 0, :], in_=a_own[:])
-        nc.vector.tensor_tensor(out=a_pair[:, 1, :], in0=a_own[:], in1=a_pair[:, 0, :], op=ALU.subtract)
+        nc.vector.reciprocal(out=a_col[:], in_=first_sum[:])
+        nc.vector.tensor_scalar(out=a_own[:], in0=own_image[:], scalar1=a_col[:, 0:1], scalar2=None, op0=ALU.mult)
+        split(a_pair[:, HI, :], a_pair[:, LO, :], a_own[:])
 
         inv_temp = keep.tile([P, 1], F32)
         nc.vector.reciprocal(out=inv_temp[:], in_=temp[:])
@@ -194,6 +211,7 @@ def tile_image_aggregation_pa_s_kernel(tc, h_cluster, w2c, b2c, scores, temperat
         quantise_h(0)
         regroup_h(2, nc.scalar.copy)
         regroup_h(3, nc.scalar.copy)
+        gt_cols = keep.tile([P, CHUNKS, BK], F32)
         nc.scalar.activation(out=gt_cols[:], in_=dm_cols[:], func=ACT.Exp, scale=inv_temp[:, 0:1])
 
         def ride_along_tensor(s):
@@ -209,7 +227,8 @@ def tile_image_aggregation_pa_s_kernel(tc, h_cluster, w2c, b2c, scores, temperat
         z_sum = keep.tile([P, CHUNKS, B], F32)
         b_vec = keep.tile([P, CHUNKS, B], F32)
         b_pair = keep.tile([P, CHUNKS, 2, B], BF16)
-        a_col = keep.tile([P, 1], F32)
+        y_sum = keep.tile([P, B], F32)
+        a_both = keep.tile([P, B], F32)
         alpha_col = keep.tile([P, 1], F32)
         ga = keep.tile([P, CHUNKS, BK], F32)
         a_rows_ps = None
@@ -223,15 +242,15 @@ def tile_image_aggregation_pa_s_kernel(tc, h_cluster, w2c, b2c, scores, temperat
             for c in range(CHUNKS):
                 nc.tensor.matmul(
                     out=z_ps[:, c].rearrange("p i b -> p (i b)"),
-                    lhsT=g_rows_pair[:, 0, c * P : (c + 1) * P],
+                    lhsT=g_rows_pair[:, HI, chunk_pixels(c)],
                     rhs=a_pair[:].rearrange("p i b -> p (i b)"),
                     start=True,
                     stop=False,
                 )
                 nc.tensor.matmul(
-                    out=z_ps[:, c, 0, :],
-                    lhsT=g_rows_pair[:, 1, c * P : (c + 1) * P],
-                    rhs=a_pair[:, 0, :],
+                    out=z_ps[:, c, HI, :],
+                    lhsT=g_rows_pair[:, LO, chunk_pixels(c)],
+                    rhs=a_pair[:, HI, :],
                     start=False,
                     stop=True,
                 )
@@ -244,49 +263,46 @@ def tile_image_aggregation_pa_s_kernel(tc, h_cluster, w2c, b2c, scores, temperat
                 )
             nc.vector.tensor_reduce(out=z_sum[:], in_=z_ps[:].rearrange("p c i b -> p c b i"), axis=AXIS_X, op=ALU.add)
             nc.vector.reciprocal(out=b_vec[:], in_=z_sum[:])
-            if last:
-                break
-            nc.vector.tensor_copy(out=b_pair[:, :, 0, :], in_=b_vec[:])
-            nc.vector.tensor_tensor(out=b_pair[:, :, 1, :], in0=b_vec[:], in1=b_pair[:, :, 0, :], op=ALU.subtract)
-            ride_along_vector(2 * r)
+            if not last:
+                split(b_pair[:, :, HI, :], b_pair[:, :, LO, :], b_vec[:])
+                ride_along_vector(2 * r)
 
-            y_ps = vecs.tile([P, 2, B], F32, tag="vec")
-            for c in range(CHUNKS):
-                nc.tensor.matmul(
-                    out=y_ps[:].rearrange("p i b -> p (i b)"),
-                    lhsT=g_cols_pair[:, 0, c, :],
-                    rhs=b_pair[:, c].rearrange("p i b -> p (i b)"),
-                    start=(c == 0),
-                    stop=False,
-                )
-                nc.tensor.matmul(
-                    out=y_ps[:, 0, :],
-                    lhsT=g_cols_pair[:, 1, c, :],
-                    rhs=b_pair[:, c, 0, :],
-                    start=False,
-                    stop=(c == CHUNKS - 1),
-                )
-            ride_along_tensor(2 * r + 1)
-            nc.vector.tensor_reduce(out=inv_sum[:], in_=y_ps[:].rearrange("p i b -> p b i"), axis=AXIS_X, op=ALU.add)
-            nc.vector.reciprocal(out=inv_sum[:], in_=inv_sum[:])
-            nc.vector.tensor_mul(out=a_own[:], in0=inv_sum[:], in1=own_image[:])
-            if r == ROUNDS - 2:
-                nc.vector.reduce_sum(out=a_col[:], in_=a_own[:], axis=AXIS_X)
-                nc.gpsimd.tensor_tensor(out=alpha_col[:], in0=a_col[:], in1=inv_temp[:], op=ALU.pow)
-            nc.vector.tensor_copy(out=a_pair[:, 0, :], in_=a_own[:])
-            nc.vector.tensor_tensor(out=a_pair[:, 1, :], in0=a_own[:], in1=a_pair[:, 0, :], op=ALU.subtract)
-            ride_along_vector(2 * r + 1)
+                y_ps = vecs.tile([P, 2, B], F32, tag="vec")
+                for c in range(CHUNKS):
+                    nc.tensor.matmul(
+                        out=y_ps[:].rearrange("p i b -> p (i b)"),
+                        lhsT=g_cols_pair[:, HI, c, :],
+                        rhs=b_pair[:, c].rearrange("p i b -> p (i b)"),
+                        start=(c == 0),
+                        stop=False,
+                    )
+                    nc.tensor.matmul(
+                        out=y_ps[:, HI, :],
+                        lhsT=g_cols_pair[:, LO, c, :],
+                        rhs=b_pair[:, c, HI, :],
+                        start=False,
+                        stop=(c == CHUNKS - 1),
+                    )
+                ride_along_tensor(2 * r + 1)
+                nc.vector.tensor_reduce(out=y_sum[:], in_=y_ps[:].rearrange("p i b -> p b i"), axis=AXIS_X, op=ALU.add)
+                nc.vector.reciprocal(out=a_both[:], in_=y_sum[:])
+                nc.vector.tensor_mul(out=a_own[:], in0=a_both[:], in1=own_image[:])
+                if r == ROUNDS - 2:
+                    nc.vector.reduce_sum(out=a_col[:], in_=a_own[:], axis=AXIS_X)
+                    nc.gpsimd.tensor_tensor(out=alpha_col[:], in0=a_col[:], in1=inv_temp[:], op=ALU.pow)
+                split(a_pair[:, HI, :], a_pair[:, LO, :], a_own[:])
+                ride_along_vector(2 * r + 1)
 
         ln_z = keep.tile([P, CHUNKS, B], F32)
         beta = keep.tile([P, CHUNKS, B], F32)
         nc.scalar.activation(out=ln_z[:], in_=z_sum[:], func=ACT.Ln)
         nc.scalar.activation(out=beta[:], in_=ln_z[:], func=ACT.Exp, scale=neg_inv_temp[:, 0:1])
-        gta = keep.tile([P, CHUNKS, BK], F32)
         plain = keep.tile([P, CHUNKS, BK], F32)
+        gta = keep.tile([P, CHUNKS, BK], F32)
         tempered = keep.tile([P, CHUNKS, BK], F32)
         nc.vector.tensor_tensor(
-            out=plain[:].rearrange("p c (b k) -> p c b k", b=B),
-            in0=ga[:].rearrange("p c (b k) -> p c b k", b=B),
+            out=by_image(plain[:]),
+            in0=by_image(ga[:]),
             in1=b_vec[:].unsqueeze(3).to_broadcast([P, CHUNKS, B, K]),
             op=ALU.mult,
         )
@@ -295,6 +311,7 @@ def tile_image_aggregation_pa_s_kernel(tc, h_cluster, w2c, b2c, scores, temperat
         )
         for b in range(B):
             quantise_f(b)
+
         p_grouped = keep.tile([P, PASSES, BK, PACK], BF16, align_bytes=64)
         p_codes = keep.tile([P, PASSES, BK], U32, align_bytes=64)
         p_scales = keep.tile([P, PASSES, BK], U8, align_bytes=64)
@@ -302,10 +319,10 @@ def tile_image_aggregation_pa_s_kernel(tc, h_cluster, w2c, b2c, scores, temperat
         for b in range(B):
             agg_ps[b] = banks.tile([P, BK], F32, tag="bank", name="agg_ps%d" % b)
         for g in range(PASSES):
-            chunks = slice(g * PACK, (g + 1) * PACK)
+            chunks = pass_chunks(g)
             nc.vector.tensor_tensor(
-                out=tempered[:, chunks, :].rearrange("p c (b k) -> p c b k", b=B),
-                in0=gta[:, chunks, :].rearrange("p c (b k) -> p c b k", b=B),
+                out=by_image(tempered[:, chunks, :]),
+                in0=by_image(gta[:, chunks, :]),
                 in1=beta[:, chunks, :].unsqueeze(3).to_broadcast([P, PACK, B, K]),
                 op=ALU.mult,
             )

@@ -21,6 +21,7 @@ PASSES = N // (P * PACK)
 PIECES = B * PASSES
 ROUNDS = 3
 HI, LO = 0, 1
+FAR = 2.0**120
 RUN = 4
 
 FLOPS = 2 * B * (D * HID * N + D * K * N)
@@ -59,10 +60,12 @@ def tile_image_aggregation_pa_s_kernel(tc, h_cluster, w2c, b2c, scores, temperat
         nc.gpsimd.memset(ones[:], 1.0)
         own_image = keep.tile([P, B], F32)
         nc.vector.memset(own_image[:], 0.0)
+        other_image = keep.tile([P, B], BF16)
+        nc.vector.memset(other_image[:], FAR)
         for b in range(B):
-            nc.vector.memset(own_image[b * K : (b + 1) * K, b : b + 1], 1.0)
-        minus_half = keep.tile([P, B], F32)
-        nc.vector.memset(minus_half[:], -0.5)
+            own = slice(b * K, (b + 1) * K)
+            nc.vector.memset(own_image[own, b : b + 1], 1.0)
+            nc.vector.memset(other_image[own, b : b + 1], 0.0)
 
         s_rows = keep.tile([P, N], BF16)
         nc.sync.dma_start(out=s_rows[:], in_=scores.rearrange("b k n -> (b k) n"))
@@ -187,16 +190,21 @@ def tile_image_aggregation_pa_s_kernel(tc, h_cluster, w2c, b2c, scores, temperat
                     nc.tensor.transpose(pair_ps[:, part, t, :], g_cols_pair[:, part, g * PACK + t, :], ident_bf[:])
             nc.scalar.copy(out=g_rows_pair[:, :, pass_pixels(g)], in_=pair_ps[:].rearrange("p i t n -> p i (t n)"))
 
-        def split(hi, lo, value):
-            nc.vector.tensor_copy(out=hi, in_=value)
-            nc.vector.tensor_tensor(out=lo, in0=value, in1=hi, op=ALU.subtract)
+        PRODUCTS = ((LO, HI), (HI, HI), (HI, LO))
+        ctx.enter_context(nc.allow_low_precision("v[HI] is v rounded to bfloat16; v[LO] holds what that leaves"))
 
         a_col = keep.tile([P, 1], F32)
         a_own = keep.tile([P, B], F32)
         a_pair = keep.tile([P, 2, B], BF16)
         nc.vector.reciprocal(out=a_col[:], in_=first_sum[:])
+        nc.vector.tensor_scalar(out=a_pair[:, HI, :], in0=own_image[:], scalar1=a_col[:, 0:1], scalar2=None, op0=ALU.mult)
         nc.vector.tensor_scalar(out=a_own[:], in0=own_image[:], scalar1=a_col[:, 0:1], scalar2=None, op0=ALU.mult)
-        split(a_pair[:, HI, :], a_pair[:, LO, :], a_own[:])
+        nc.vector.tensor_tensor(out=a_pair[:, LO, :], in0=a_own[:], in1=a_pair[:, HI, :], op=ALU.subtract)
+
+        def reciprocal_pair(hi, lo, value, sums):
+            nc.vector.reciprocal(out=hi, in_=sums)
+            nc.vector.reciprocal(out=value, in_=sums)
+            nc.vector.tensor_tensor(out=lo, in0=value, in1=hi, op=ALU.subtract)
 
         inv_temp = keep.tile([P, 1], F32)
         nc.vector.reciprocal(out=inv_temp[:], in_=temp[:])
@@ -224,36 +232,28 @@ def tile_image_aggregation_pa_s_kernel(tc, h_cluster, w2c, b2c, scores, temperat
             if s < PIECES:
                 add_bias(s)
 
-        z_sum = keep.tile([P, CHUNKS, B], F32)
         b_vec = keep.tile([P, CHUNKS, B], F32)
-        b_pair = keep.tile([P, CHUNKS, 2, B], BF16)
-        y_sum = keep.tile([P, B], F32)
-        a_both = keep.tile([P, B], F32)
+        b_pair = keep.tile([P, 2, CHUNKS, B], BF16)
         alpha_col = keep.tile([P, 1], F32)
         ga = keep.tile([P, CHUNKS, BK], F32)
         a_rows_ps = None
         alpha_rows_ps = None
+        z_ps = None
         for r in range(ROUNDS):
             last = r == ROUNDS - 1
             if last:
                 a_rows_ps = vecs.tile([P, BK], F32, tag="vec")
                 nc.tensor.transpose(a_rows_ps[:], a_col[:, 0:1].to_broadcast([P, P]), ident[:])
-            z_ps = vecs.tile([P, CHUNKS, 2, B], F32, tag="vec")
-            for c in range(CHUNKS):
-                nc.tensor.matmul(
-                    out=z_ps[:, c].rearrange("p i b -> p (i b)"),
-                    lhsT=g_rows_pair[:, HI, chunk_pixels(c)],
-                    rhs=a_pair[:].rearrange("p i b -> p (i b)"),
-                    start=True,
-                    stop=False,
-                )
-                nc.tensor.matmul(
-                    out=z_ps[:, c, HI, :],
-                    lhsT=g_rows_pair[:, LO, chunk_pixels(c)],
-                    rhs=a_pair[:, HI, :],
-                    start=False,
-                    stop=True,
-                )
+            z_ps = vecs.tile([P, CHUNKS, B], F32, tag="vec")
+            for i, (g_part, v_part) in enumerate(PRODUCTS):
+                for c in range(CHUNKS):
+                    nc.tensor.matmul(
+                        out=z_ps[:, c, :],
+                        lhsT=g_rows_pair[:, g_part, chunk_pixels(c)],
+                        rhs=a_pair[:, v_part, :],
+                        start=(i == 0 and c == 0),
+                        stop=(i == len(PRODUCTS) - 1 and c == CHUNKS - 1),
+                    )
             ride_along_tensor(2 * r)
             if last:
                 alpha_rows_ps = vecs.tile([P, BK], F32, tag="vec")
@@ -261,42 +261,35 @@ def tile_image_aggregation_pa_s_kernel(tc, h_cluster, w2c, b2c, scores, temperat
                 nc.vector.tensor_tensor(
                     out=ga[:], in0=g_cols[:], in1=a_rows_ps[:].unsqueeze(1).to_broadcast([P, CHUNKS, BK]), op=ALU.mult
                 )
-            nc.vector.tensor_reduce(out=z_sum[:], in_=z_ps[:].rearrange("p c i b -> p c b i"), axis=AXIS_X, op=ALU.add)
-            nc.vector.reciprocal(out=b_vec[:], in_=z_sum[:])
-            if not last:
-                split(b_pair[:, :, HI, :], b_pair[:, :, LO, :], b_vec[:])
+                nc.vector.reciprocal(out=b_vec[:], in_=z_ps[:])
+            else:
+                reciprocal_pair(b_pair[:, HI], b_pair[:, LO], b_vec[:], z_ps[:])
                 ride_along_vector(2 * r)
 
-                y_ps = vecs.tile([P, 2, B], F32, tag="vec")
-                for c in range(CHUNKS):
-                    nc.tensor.matmul(
-                        out=y_ps[:].rearrange("p i b -> p (i b)"),
-                        lhsT=g_cols_pair[:, HI, c, :],
-                        rhs=b_pair[:, c].rearrange("p i b -> p (i b)"),
-                        start=(c == 0),
-                        stop=False,
-                    )
-                    nc.tensor.matmul(
-                        out=y_ps[:, HI, :],
-                        lhsT=g_cols_pair[:, LO, c, :],
-                        rhs=b_pair[:, c, HI, :],
-                        start=False,
-                        stop=(c == CHUNKS - 1),
-                    )
+                y_ps = vecs.tile([P, B], F32, tag="vec")
+                nc.tensor.matmul(out=y_ps[:], lhsT=ident_bf[:], rhs=other_image[:], start=True, stop=False)
+                for i, (g_part, v_part) in enumerate(PRODUCTS):
+                    for c in range(CHUNKS):
+                        nc.tensor.matmul(
+                            out=y_ps[:],
+                            lhsT=g_cols_pair[:, g_part, c, :],
+                            rhs=b_pair[:, v_part, c, :],
+                            start=False,
+                            stop=(i == len(PRODUCTS) - 1 and c == CHUNKS - 1),
+                        )
                 ride_along_tensor(2 * r + 1)
-                nc.vector.tensor_reduce(out=y_sum[:], in_=y_ps[:].rearrange("p i b -> p b i"), axis=AXIS_X, op=ALU.add)
-                nc.vector.reciprocal(out=a_both[:], in_=y_sum[:])
-                nc.vector.tensor_mul(out=a_own[:], in0=a_both[:], in1=own_image[:])
+                reciprocal_pair(a_pair[:, HI], a_pair[:, LO], a_own[:], y_ps[:])
                 if r == ROUNDS - 2:
                     nc.vector.reduce_sum(out=a_col[:], in_=a_own[:], axis=AXIS_X)
                     nc.gpsimd.tensor_tensor(out=alpha_col[:], in0=a_col[:], in1=inv_temp[:], op=ALU.pow)
-                split(a_pair[:, HI, :], a_pair[:, LO, :], a_own[:])
                 ride_along_vector(2 * r + 1)
 
         ln_z = keep.tile([P, CHUNKS, B], F32)
         beta = keep.tile([P, CHUNKS, B], F32)
-        nc.scalar.activation(out=ln_z[:], in_=z_sum[:], func=ACT.Ln)
+        nc.scalar.activation(out=ln_z[:], in_=z_ps[:], func=ACT.Ln)
         nc.scalar.activation(out=beta[:], in_=ln_z[:], func=ACT.Exp, scale=neg_inv_temp[:, 0:1])
+        table_ready = keep.tile([P, 1], F32)
+        nc.scalar.activation(out=table_ready[:], in_=inv_temp[:], func=ACT.Abs_reciprocal_sqrt)
         plain = keep.tile([P, CHUNKS, BK], F32)
         gta = keep.tile([P, CHUNKS, BK], F32)
         tempered = keep.tile([P, CHUNKS, BK], F32)
@@ -359,17 +352,16 @@ def tile_image_aggregation_pa_s_kernel(tc, h_cluster, w2c, b2c, scores, temperat
             )
         total_ps = vecs.tile([P, B], F32, tag="vec")
         nc.tensor.matmul(out=total_ps[:], lhsT=ones[:], rhs=square_sums[:], start=True, stop=True)
-        clamped = keep.tile([P, B], F32)
-        nc.vector.tensor_scalar_max(out=clamped[:], in0=total_ps[:], scalar1=1e-24)
         inv_norm = keep.tile([P, B], F32)
-        nc.gpsimd.tensor_tensor(out=inv_norm[:], in0=clamped[:], in1=minus_half[:], op=ALU.pow)
+        nc.scalar.activation(out=inv_norm[:], in_=total_ps[:], func=ACT.Abs_reciprocal_sqrt)
         result = keep.tile([P, B, K], F32)
         for b in range(B):
-            nc.vector.tensor_scalar(
+            nc.vector.scalar_tensor_tensor(
                 out=result[:, b, :],
-                in0=agg_ps[b][:, b * K : (b + 1) * K],
-                scalar1=inv_norm[:, b : b + 1],
-                scalar2=None,
-                op0=ALU.mult,
+                in0=inv_norm[:, b : b + 1].to_broadcast([P, K]),
+                scalar=1e12,
+                in1=agg_ps[b][:, b * K : (b + 1) * K],
+                op0=ALU.min,
+                op1=ALU.mult,
             )
         nc.sync.dma_start(out=out.rearrange("b (d k) -> d b k", k=K), in_=result[:])

@@ -39,6 +39,10 @@ def chunk_pixels(c):
     return slice(c * P, (c + 1) * P)
 
 
+def image_clusters(b):
+    return slice(b * K, (b + 1) * K)
+
+
 def by_image(cols):
     return cols.rearrange("p c (b k) -> p c b k", b=B)
 
@@ -48,9 +52,9 @@ def tile_image_aggregation_pa_s_kernel(tc, h_cluster, w2c, b2c, scores, temperat
     with ExitStack() as ctx:
         ctx.enter_context(tc.manual_schedule())
         keep = ctx.enter_context(tc.tile_pool(name="keep", bufs=1))
-        banks = ctx.enter_context(tc.psum_pool(name="banks", bufs=4))
+        stay = ctx.enter_context(tc.psum_pool(name="stay", bufs=1))
+        banks = ctx.enter_context(tc.psum_pool(name="banks", bufs=3))
         vecs = ctx.enter_context(tc.psum_pool(name="vecs", bufs=3))
-        lone = ctx.enter_context(tc.psum_pool(name="lone", bufs=1))
 
         ident = keep.tile([P, P], F32)
         make_identity(nc, ident[:])
@@ -144,40 +148,63 @@ def tile_image_aggregation_pa_s_kernel(tc, h_cluster, w2c, b2c, scores, temperat
                 out=d_rows[:, pass_pixels(g)],
                 in0=s_rows[:, pass_pixels(g)],
                 scalar1=rowmax[:, 0:1],
-                scalar2=None,
+                scalar2=-1.0,
                 op0=ALU.subtract,
+                op1=ALU.mult,
             )
-            d_cols_ps[g] = banks.tile([P, PACK, BK], F32, tag="bank", name="d_cols_ps%d" % g)
+            d_cols_ps[g] = stay.tile([P, PACK, BK], F32, name="d_cols_ps%d" % g)
             for t in range(PACK):
                 nc.tensor.transpose(d_cols_ps[g][:, t, :], d_rows[:, chunk_pixels(g * PACK + t)], ident[:])
+        inv_temp = keep.tile([P, 1], F32)
+        nc.vector.reciprocal(out=inv_temp[:], in_=temp[:])
+        neg_inv_temp = keep.tile([P, 1], F32)
+        nc.vector.tensor_scalar_mul(out=neg_inv_temp[:], in0=inv_temp[:], scalar1=-1.0)
 
         exp_rows = keep.tile([P, N], BF16)
         first_sum = keep.tile([P, 1], F32)
-        nc.scalar.activation(out=exp_rows[:], in_=d_rows[:], func=ACT.Exp, accum_out=first_sum[:])
+        nc.scalar.activation(out=exp_rows[:], in_=d_rows[:], func=ACT.Exp, scale=-1.0, accum_out=first_sum[:])
 
         w_words = w_rows[:].bitcast(F32).rearrange("d (p u) -> d u p", u=2)
-        w_ps = lone.tile([P, 2, D], F32)
+        w_ps = banks.tile([P, 2, D], F32, tag="bank")
         for u in range(2):
             nc.tensor.transpose(w_ps[:, u, :], w_words[:, u, :], ident[:])
 
-        colmax = keep.tile([P, CHUNKS, B], F32)
-        dm_cols = keep.tile([P, CHUNKS, BK], F32)
+        colmin = keep.tile([P, CHUNKS, B], F32)
+        colmin_t = keep.tile([P, CHUNKS, B], F32)
         g_cols = keep.tile([P, CHUNKS, BK], F32)
         g_cols_pair = keep.tile([P, 2, CHUNKS, BK], BF16)
         g_rows_pair = keep.tile([P, 2, N], BF16)
         for g in range(PASSES):
             chunks = pass_chunks(g)
-            nc.vector.tensor_reduce(out=colmax[:, chunks, :], in_=by_image(d_cols_ps[g][:]), axis=AXIS_X, op=ALU.max)
-            nc.vector.tensor_tensor(
-                out=by_image(dm_cols[:, chunks, :]),
-                in0=by_image(d_cols_ps[g][:]),
-                in1=colmax[:, chunks, :].unsqueeze(3).to_broadcast([P, PACK, B, K]),
-                op=ALU.subtract,
-            )
-            nc.scalar.activation(out=g_cols[:, chunks, :], in_=dm_cols[:, chunks, :], func=ACT.Exp)
-            nc.scalar.activation(out=g_cols_pair[:, HI, chunks, :], in_=dm_cols[:, chunks, :], func=ACT.Exp)
+            nc.vector.tensor_reduce(out=colmin[:, chunks, :], in_=by_image(d_cols_ps[g][:]), axis=AXIS_X, op=ALU.min)
+            for t in range(PACK):
+                for b in range(B):
+                    nc.scalar.activation(
+                        out=g_cols[:, g * PACK + t, image_clusters(b)],
+                        in_=d_cols_ps[g][:, t, image_clusters(b)],
+                        func=ACT.Exp,
+                        scale=-1.0,
+                        bias=colmin[:, g * PACK + t, b : b + 1],
+                    )
+
+        a_col = keep.tile([P, 1], F32)
+        a_own = keep.tile([P, B], F32)
+        a_pair = keep.tile([P, 2, B], BF16)
+        nc.vector.reciprocal(out=a_col[:], in_=first_sum[:])
+        nc.vector.tensor_scalar(out=a_pair[:, HI, :], in0=own_image[:], scalar1=a_col[:, 0:1], scalar2=None, op0=ALU.mult)
+        nc.vector.tensor_scalar(out=a_own[:], in0=own_image[:], scalar1=a_col[:, 0:1], scalar2=None, op0=ALU.mult)
+        nc.vector.tensor_scalar(
+            out=colmin_t[:].rearrange("p c b -> p (c b)"),
+            in0=colmin[:].rearrange("p c b -> p (c b)"),
+            scalar1=inv_temp[:, 0:1],
+            scalar2=None,
+            op0=ALU.mult,
+        )
+        nc.vector.tensor_tensor(out=a_pair[:, LO, :], in0=a_own[:], in1=a_pair[:, HI, :], op=ALU.subtract)
+
         for g in range(PASSES):
             chunks = pass_chunks(g)
+            nc.vector.tensor_copy(out=g_cols_pair[:, HI, chunks, :], in_=g_cols[:, chunks, :])
             nc.vector.tensor_tensor(
                 out=g_cols_pair[:, LO, chunks, :],
                 in0=g_cols[:, chunks, :],
@@ -193,23 +220,11 @@ def tile_image_aggregation_pa_s_kernel(tc, h_cluster, w2c, b2c, scores, temperat
         PRODUCTS = ((LO, HI), (HI, HI), (HI, LO))
         ctx.enter_context(nc.allow_low_precision("v[HI] is v rounded to bfloat16; v[LO] holds what that leaves"))
 
-        a_col = keep.tile([P, 1], F32)
-        a_own = keep.tile([P, B], F32)
-        a_pair = keep.tile([P, 2, B], BF16)
-        nc.vector.reciprocal(out=a_col[:], in_=first_sum[:])
-        nc.vector.tensor_scalar(out=a_pair[:, HI, :], in0=own_image[:], scalar1=a_col[:, 0:1], scalar2=None, op0=ALU.mult)
-        nc.vector.tensor_scalar(out=a_own[:], in0=own_image[:], scalar1=a_col[:, 0:1], scalar2=None, op0=ALU.mult)
-        nc.vector.tensor_tensor(out=a_pair[:, LO, :], in0=a_own[:], in1=a_pair[:, HI, :], op=ALU.subtract)
-
         def reciprocal_pair(hi, lo, value, sums):
             nc.vector.reciprocal(out=hi, in_=sums)
             nc.vector.reciprocal(out=value, in_=sums)
             nc.vector.tensor_tensor(out=lo, in0=value, in1=hi, op=ALU.subtract)
 
-        inv_temp = keep.tile([P, 1], F32)
-        nc.vector.reciprocal(out=inv_temp[:], in_=temp[:])
-        neg_inv_temp = keep.tile([P, 1], F32)
-        nc.vector.tensor_scalar_mul(out=neg_inv_temp[:], in0=inv_temp[:], scalar1=-1.0)
         nc.vector.tensor_copy(
             out=w_grouped[:].bitcast(F32).rearrange("p (d u) -> p d u", u=2), in_=w_ps[:].rearrange("p u d -> p d u")
         )
@@ -219,8 +234,6 @@ def tile_image_aggregation_pa_s_kernel(tc, h_cluster, w2c, b2c, scores, temperat
         quantise_h(0)
         regroup_h(2, nc.scalar.copy)
         regroup_h(3, nc.scalar.copy)
-        gt_cols = keep.tile([P, CHUNKS, BK], F32)
-        nc.scalar.activation(out=gt_cols[:], in_=dm_cols[:], func=ACT.Exp, scale=inv_temp[:, 0:1])
 
         def ride_along_tensor(s):
             if s < PIECES:
@@ -231,37 +244,45 @@ def tile_image_aggregation_pa_s_kernel(tc, h_cluster, w2c, b2c, scores, temperat
                 quantise_h(s + 1)
             if s < PIECES:
                 add_bias(s)
+            if s == PIECES - 1:
+                quantise_f(0)
 
         b_vec = keep.tile([P, CHUNKS, B], F32)
         b_pair = keep.tile([P, 2, CHUNKS, B], BF16)
-        alpha_col = keep.tile([P, 1], F32)
+        ln_a_col = keep.tile([P, 1], F32)
         ga = keep.tile([P, CHUNKS, BK], F32)
+        ln_a_rows = keep.tile([P, BK], F32)
         a_rows_ps = None
-        alpha_rows_ps = None
+        ln_a_rows_ps = None
         z_ps = None
         for r in range(ROUNDS):
             last = r == ROUNDS - 1
-            if last:
-                a_rows_ps = vecs.tile([P, BK], F32, tag="vec")
-                nc.tensor.transpose(a_rows_ps[:], a_col[:, 0:1].to_broadcast([P, P]), ident[:])
             z_ps = vecs.tile([P, CHUNKS, B], F32, tag="vec")
-            for i, (g_part, v_part) in enumerate(PRODUCTS):
-                for c in range(CHUNKS):
-                    nc.tensor.matmul(
-                        out=z_ps[:, c, :],
-                        lhsT=g_rows_pair[:, g_part, chunk_pixels(c)],
-                        rhs=a_pair[:, v_part, :],
-                        start=(i == 0 and c == 0),
-                        stop=(i == len(PRODUCTS) - 1 and c == CHUNKS - 1),
-                    )
+            order = [(i, c) for i in range(len(PRODUCTS)) for c in range(CHUNKS)]
+            if r == 0:
+                order.sort(key=lambda ic: ic[1] // PACK)
+            for i, c in order:
+                g_part, v_part = PRODUCTS[i]
+                if last and (i, c) == (1, 0):
+                    a_rows_ps = vecs.tile([P, BK], F32, tag="vec")
+                    nc.tensor.transpose(a_rows_ps[:], a_col[:, 0:1].to_broadcast([P, P]), ident[:])
+                if last and (i, c) == (2, 0):
+                    ln_a_rows_ps = vecs.tile([P, BK], F32, tag="vec")
+                    nc.tensor.transpose(ln_a_rows_ps[:], ln_a_col[:, 0:1].to_broadcast([P, P]), ident[:])
+                nc.tensor.matmul(
+                    out=z_ps[:, c, :],
+                    lhsT=g_rows_pair[:, g_part, chunk_pixels(c)],
+                    rhs=a_pair[:, v_part, :],
+                    start=((i, c) == order[0]),
+                    stop=((i, c) == order[-1]),
+                )
             ride_along_tensor(2 * r)
             if last:
-                alpha_rows_ps = vecs.tile([P, BK], F32, tag="vec")
-                nc.tensor.transpose(alpha_rows_ps[:], alpha_col[:, 0:1].to_broadcast([P, P]), ident[:])
+                nc.scalar.copy(out=ln_a_rows[:], in_=ln_a_rows_ps[:])
                 nc.vector.tensor_tensor(
                     out=ga[:], in0=g_cols[:], in1=a_rows_ps[:].unsqueeze(1).to_broadcast([P, CHUNKS, BK]), op=ALU.mult
                 )
-                nc.vector.reciprocal(out=b_vec[:], in_=z_ps[:])
+                quantise_f(1)
             else:
                 reciprocal_pair(b_pair[:, HI], b_pair[:, LO], b_vec[:], z_ps[:])
                 ride_along_vector(2 * r)
@@ -281,29 +302,52 @@ def tile_image_aggregation_pa_s_kernel(tc, h_cluster, w2c, b2c, scores, temperat
                 reciprocal_pair(a_pair[:, HI], a_pair[:, LO], a_own[:], y_ps[:])
                 if r == ROUNDS - 2:
                     nc.vector.reduce_sum(out=a_col[:], in_=a_own[:], axis=AXIS_X)
-                    nc.gpsimd.tensor_tensor(out=alpha_col[:], in0=a_col[:], in1=inv_temp[:], op=ALU.pow)
+                    nc.scalar.activation(out=ln_a_col[:], in_=a_col[:], func=ACT.Ln)
                 ride_along_vector(2 * r + 1)
 
         ln_z = keep.tile([P, CHUNKS, B], F32)
-        beta = keep.tile([P, CHUNKS, B], F32)
         nc.scalar.activation(out=ln_z[:], in_=z_ps[:], func=ACT.Ln)
-        nc.scalar.activation(out=beta[:], in_=ln_z[:], func=ACT.Exp, scale=neg_inv_temp[:, 0:1])
+        nc.vector.reciprocal(out=b_vec[:], in_=z_ps[:])
+        log_ga = keep.tile([P, CHUNKS, BK], F32)
+        ln_beta = keep.tile([P, CHUNKS, B], F32)
+        plain = keep.tile([P, CHUNKS, BK], F32)
+        tempered = keep.tile([P, CHUNKS, BK], F32)
+        for g in range(PASSES):
+            chunks = pass_chunks(g)
+            nc.vector.tensor_tensor(
+                out=log_ga[:, chunks, :],
+                in0=ln_a_rows[:].unsqueeze(1).to_broadcast([P, PACK, BK]),
+                in1=d_cols_ps[g][:],
+                op=ALU.subtract,
+            )
+            if g == 0:
+                nc.vector.scalar_tensor_tensor(
+                    out=ln_beta[:].rearrange("p c b -> p (c b)"),
+                    in0=ln_z[:].rearrange("p c b -> p (c b)"),
+                    scalar=neg_inv_temp[:, 0:1],
+                    in1=colmin_t[:].rearrange("p c b -> p (c b)"),
+                    op0=ALU.mult,
+                    op1=ALU.add,
+                )
+        for c in range(CHUNKS):
+            for b in range(B):
+                nc.scalar.activation(
+                    out=tempered[:, c, image_clusters(b)],
+                    in_=log_ga[:, c, image_clusters(b)],
+                    func=ACT.Exp,
+                    scale=inv_temp[:, 0:1],
+                    bias=ln_beta[:, c, b : b + 1],
+                )
         table_ready = keep.tile([P, 1], F32)
         nc.scalar.activation(out=table_ready[:], in_=inv_temp[:], func=ACT.Abs_reciprocal_sqrt)
-        plain = keep.tile([P, CHUNKS, BK], F32)
-        gta = keep.tile([P, CHUNKS, BK], F32)
-        tempered = keep.tile([P, CHUNKS, BK], F32)
-        nc.vector.tensor_tensor(
-            out=by_image(plain[:]),
-            in0=by_image(ga[:]),
-            in1=b_vec[:].unsqueeze(3).to_broadcast([P, CHUNKS, B, K]),
-            op=ALU.mult,
-        )
-        nc.vector.tensor_tensor(
-            out=gta[:], in0=gt_cols[:], in1=alpha_rows_ps[:].unsqueeze(1).to_broadcast([P, CHUNKS, BK]), op=ALU.mult
-        )
-        for b in range(B):
-            quantise_f(b)
+        for g in range(PASSES):
+            chunks = pass_chunks(g)
+            nc.vector.tensor_tensor(
+                out=by_image(plain[:, chunks, :]),
+                in0=by_image(ga[:, chunks, :]),
+                in1=b_vec[:, chunks, :].unsqueeze(3).to_broadcast([P, PACK, B, K]),
+                op=ALU.mult,
+            )
 
         p_grouped = keep.tile([P, PASSES, BK, PACK], BF16, align_bytes=64)
         p_codes = keep.tile([P, PASSES, BK], U32, align_bytes=64)
@@ -313,12 +357,6 @@ def tile_image_aggregation_pa_s_kernel(tc, h_cluster, w2c, b2c, scores, temperat
             agg_ps[b] = banks.tile([P, BK], F32, tag="bank", name="agg_ps%d" % b)
         for g in range(PASSES):
             chunks = pass_chunks(g)
-            nc.vector.tensor_tensor(
-                out=by_image(tempered[:, chunks, :]),
-                in0=by_image(gta[:, chunks, :]),
-                in1=beta[:, chunks, :].unsqueeze(3).to_broadcast([P, PACK, B, K]),
-                op=ALU.mult,
-            )
             nc.vector.tensor_tensor(
                 out=p_grouped[:, g],
                 in0=plain[:, chunks, :].rearrange("p t m -> p m t"),

@@ -62,6 +62,8 @@ def tile_image_aggregation_pa_s_kernel(tc, h_cluster, w2c, b2c, scores, temperat
         make_identity(nc, ident_bf[:])
         ones = keep.tile([P, P], F32)
         nc.gpsimd.memset(ones[:], 1.0)
+        ones_bf = keep.tile([P, P], BF16)
+        nc.gpsimd.memset(ones_bf[:], 1.0)
         own_image = keep.tile([P, B], F32)
         nc.vector.memset(own_image[:], 0.0)
         other_image = keep.tile([P, B], BF16)
@@ -73,15 +75,19 @@ def tile_image_aggregation_pa_s_kernel(tc, h_cluster, w2c, b2c, scores, temperat
 
         s_rows = keep.tile([P, N], BF16)
         nc.sync.dma_start(out=s_rows[:], in_=scores.rearrange("b k n -> (b k) n"))
-        temp = keep.tile([P, 1], BF16)
-        nc.sync.dma_start(out=temp[:], in_=temperature.partition_broadcast(P))
+        row_bf = keep.tile([P, D + 2], BF16)
+        nc.vector.memset(row_bf[:], 0.0)
+        nc.scalar.dma_start(out=row_bf[0:1, 0:D], in_=b2c.unsqueeze(0))
+        nc.scalar.dma_start(out=row_bf[0:1, D : D + 1], in_=temperature.unsqueeze(0))
         w_rows = keep.tile([P, HID], BF16)
         nc.sync.dma_start(out=w_rows[:], in_=w2c)
-        bias_rows = keep.tile([P, D], BF16)
-        nc.sync.dma_start(out=bias_rows[:], in_=b2c.partition_broadcast(P))
-        h_raw = keep.tile([P, B, PACK, N], BF16)
-        for b in range(B):
-            nc.sync.dma_start(out=h_raw[:, b], in_=h_cluster[b].rearrange("(p j) n -> p j n", j=PACK))
+        h_raw = keep.tile([P, PIECES, PACK, P * PACK], BF16)
+        for q in range(PIECES):
+            b, g = q % B, q // B
+            nc.sync.dma_start(
+                out=h_raw[:, q],
+                in_=h_cluster[b].rearrange("(p j) n -> p j n", j=PACK)[:, :, pass_pixels(g)],
+            )
 
         w_grouped = keep.tile([P, D * PACK], BF16, align_bytes=64)
         w_codes = keep.tile([P, D], U32, align_bytes=64)
@@ -98,7 +104,7 @@ def tile_image_aggregation_pa_s_kernel(tc, h_cluster, w2c, b2c, scores, temperat
             b, g = q % B, q // B
             copy(
                 out=h_grouped[:, b, pass_pixels(g), :].rearrange("p (c i) j -> p c j i", i=RUN),
-                in_=h_raw[:, b, :, pass_pixels(g)].rearrange("p j (c i) -> p c j i", i=RUN),
+                in_=h_raw[:, q].rearrange("p j (c i) -> p c j i", i=RUN),
             )
 
         def quantise_h(q):
@@ -155,10 +161,6 @@ def tile_image_aggregation_pa_s_kernel(tc, h_cluster, w2c, b2c, scores, temperat
             d_cols_ps[g] = stay.tile([P, PACK, BK], F32, name="d_cols_ps%d" % g)
             for t in range(PACK):
                 nc.tensor.transpose(d_cols_ps[g][:, t, :], d_rows[:, chunk_pixels(g * PACK + t)], ident[:])
-        inv_temp = keep.tile([P, 1], F32)
-        nc.vector.reciprocal(out=inv_temp[:], in_=temp[:])
-        neg_inv_temp = keep.tile([P, 1], F32)
-        nc.vector.tensor_scalar_mul(out=neg_inv_temp[:], in0=inv_temp[:], scalar1=-1.0)
 
         exp_rows = keep.tile([P, N], BF16)
         first_sum = keep.tile([P, 1], F32)
@@ -166,6 +168,9 @@ def tile_image_aggregation_pa_s_kernel(tc, h_cluster, w2c, b2c, scores, temperat
 
         w_words = w_rows[:].bitcast(F32).rearrange("d (p u) -> d u p", u=2)
         w_ps = banks.tile([P, 2, D], F32, tag="bank")
+        spread_ps = vecs.tile([P, D + 2], F32, tag="vec")
+        nc.tensor.matmul(out=spread_ps[:], lhsT=ones_bf[:], rhs=row_bf[:], start=True, stop=True)
+        bias_rows = keep.tile([P, D], F32)
         for u in range(2):
             nc.tensor.transpose(w_ps[:, u, :], w_words[:, u, :], ident[:])
 
@@ -187,19 +192,14 @@ def tile_image_aggregation_pa_s_kernel(tc, h_cluster, w2c, b2c, scores, temperat
                         bias=colmin[:, g * PACK + t, b : b + 1],
                     )
 
+        nc.scalar.copy(out=bias_rows[:], in_=spread_ps[:, 0:D])
+
         a_col = keep.tile([P, 1], F32)
         a_own = keep.tile([P, B], F32)
         a_pair = keep.tile([P, 2, B], BF16)
         nc.vector.reciprocal(out=a_col[:], in_=first_sum[:])
         nc.vector.tensor_scalar(out=a_pair[:, HI, :], in0=own_image[:], scalar1=a_col[:, 0:1], scalar2=None, op0=ALU.mult)
         nc.vector.tensor_scalar(out=a_own[:], in0=own_image[:], scalar1=a_col[:, 0:1], scalar2=None, op0=ALU.mult)
-        nc.vector.tensor_scalar(
-            out=colmin_t[:].rearrange("p c b -> p (c b)"),
-            in0=colmin[:].rearrange("p c b -> p (c b)"),
-            scalar1=inv_temp[:, 0:1],
-            scalar2=None,
-            op0=ALU.mult,
-        )
         nc.vector.tensor_tensor(out=a_pair[:, LO, :], in0=a_own[:], in1=a_pair[:, HI, :], op=ALU.subtract)
 
         for g in range(PASSES):
@@ -228,7 +228,16 @@ def tile_image_aggregation_pa_s_kernel(tc, h_cluster, w2c, b2c, scores, temperat
         nc.vector.tensor_copy(
             out=w_grouped[:].bitcast(F32).rearrange("p (d u) -> p d u", u=2), in_=w_ps[:].rearrange("p u d -> p d u")
         )
+        inv_temp = keep.tile([P, 1], F32)
+        neg_inv_temp = keep.tile([P, 1], F32)
+        nc.vector.reciprocal(out=inv_temp[:], in_=spread_ps[:, D : D + 1])
         regroup_h(0, nc.vector.tensor_copy)
+        nc.vector.tensor_scalar_mul(out=neg_inv_temp[:], in0=inv_temp[:], scalar1=-1.0)
+        nc.vector.tensor_scalar_mul(
+            out=colmin_t[:].rearrange("p c b -> p (c b)"),
+            in0=colmin[:].rearrange("p c b -> p (c b)"),
+            scalar1=inv_temp[:, 0:1],
+        )
         nc.vector.quantize_mx(out=w_codes[:].bitcast(FP8X4), scales=w_scales[:], in_=w_grouped[:])
         regroup_h(1, nc.vector.tensor_copy)
         quantise_h(0)

@@ -24,6 +24,8 @@ HI, LO = 0, 1
 FAR = 2.0**120
 RUN = 4
 
+DUMMIES = (1, 1, 1, 0)
+PRODUCT_CHUNKS = 6
 FLOPS = 2 * B * (D * HID * N + D * K * N)
 
 
@@ -52,10 +54,11 @@ def tile_image_aggregation_pa_s_kernel(tc, h_cluster, w2c, b2c, scores, temperat
     with ExitStack() as ctx:
         ctx.enter_context(tc.manual_schedule())
         keep = ctx.enter_context(tc.tile_pool(name="keep", bufs=1))
-        stay = ctx.enter_context(tc.psum_pool(name="stay", bufs=1))
-        banks = ctx.enter_context(tc.psum_pool(name="banks", bufs=3))
+        banks = ctx.enter_context(tc.psum_pool(name="banks", bufs=5))
         vecs = ctx.enter_context(tc.psum_pool(name="vecs", bufs=3))
 
+        row_bf = keep.tile([P, D + 2], BF16)
+        nc.vector.memset(row_bf[:], 0.0)
         ident = keep.tile([P, P], F32)
         make_identity(nc, ident[:])
         ident_bf = keep.tile([P, P], BF16)
@@ -75,8 +78,6 @@ def tile_image_aggregation_pa_s_kernel(tc, h_cluster, w2c, b2c, scores, temperat
 
         s_rows = keep.tile([P, N], BF16)
         nc.sync.dma_start(out=s_rows[:], in_=scores.rearrange("b k n -> (b k) n"))
-        row_bf = keep.tile([P, D + 2], BF16)
-        nc.vector.memset(row_bf[:], 0.0)
         nc.scalar.dma_start(out=row_bf[0:1, 0:D], in_=b2c.unsqueeze(0))
         nc.scalar.dma_start(out=row_bf[0:1, D : D + 1], in_=temperature.unsqueeze(0))
         w_rows = keep.tile([P, HID], BF16)
@@ -95,10 +96,12 @@ def tile_image_aggregation_pa_s_kernel(tc, h_cluster, w2c, b2c, scores, temperat
         h_grouped = keep.tile([P, B, N, PACK], BF16, align_bytes=64)
         h_codes = keep.tile([P, B, N], U32, align_bytes=64)
         h_scales = keep.tile([P, B, N], U8, align_bytes=64)
-        f_grouped = keep.tile([P, B, PASSES, D, PACK], BF16, align_bytes=64)
+        f_rows = keep.tile([P, PIECES, P * PACK], BF16, align_bytes=64)
+        f_grouped = keep.tile([P, B, PASSES, D * PACK], BF16, align_bytes=64)
         f_codes = keep.tile([P, B, PASSES, D], U32, align_bytes=64)
         f_scales = keep.tile([P, B, PASSES, D], U8, align_bytes=64)
         f_ps = {}
+        f_turned_ps = {}
 
         def regroup_h(q, copy):
             b, g = q % B, q // B
@@ -117,32 +120,39 @@ def tile_image_aggregation_pa_s_kernel(tc, h_cluster, w2c, b2c, scores, temperat
 
         def multiply_f(q):
             b, g = q % B, q // B
-            f_ps[q] = banks.tile([P, PACK, D], F32, tag="bank", name="f_ps%d" % q)
-            for t in range(PACK):
-                nc.tensor.matmul_mx(
-                    out=f_ps[q][:, t, :],
-                    lhsT=h_codes[:, b, chunk_pixels(g * PACK + t)].bitcast(FP8X4),
-                    lhsT_scale=h_scales[:, b, chunk_pixels(g * PACK + t)],
-                    rhs=w_codes[:].bitcast(FP8X4),
-                    rhs_scale=w_scales[:],
-                    start=True,
-                    stop=True,
-                )
+            f_ps[q] = banks.tile([P, P * PACK], F32, tag="bank", name="f_ps%d" % q)
+            for repeat in range(DUMMIES[q] + 1):
+              nc.tensor.matmul_mx(
+                out=f_ps[q][:],
+                lhsT=w_codes[:].bitcast(FP8X4),
+                lhsT_scale=w_scales[:],
+                rhs=h_codes[:, b, pass_pixels(g)].bitcast(FP8X4),
+                rhs_scale=h_scales[:, b, pass_pixels(g)],
+                start=True,
+                stop=True,
+            )
 
         def add_bias(q):
+            nc.scalar.activation(out=f_rows[:, q], in_=f_ps[q][:], func=ACT.Identity, bias=bias_col[:, 0:1])
+
+        def turn_f(q):
+            f_turned_ps[q] = banks.tile([P, 2, D], F32, tag="bank", name="f_turned_ps%d" % q)
+            words = f_rows[:, q].bitcast(F32)
+            for u in range(2):
+                nc.tensor.transpose(f_turned_ps[q][:, u, :], words[:, u * P : (u + 1) * P], ident[:])
+
+        def group_f(q, copy):
             b, g = q % B, q // B
-            nc.vector.tensor_tensor(
-                out=f_grouped[:, b, g],
-                in0=f_ps[q][:].rearrange("p t d -> p d t"),
-                in1=bias_rows[:].unsqueeze(2).to_broadcast([P, D, PACK]),
-                op=ALU.add,
+            copy(
+                out=f_grouped[:, b, g].bitcast(F32).rearrange("p (d u) -> p d u", u=2),
+                in_=f_turned_ps[q][:].rearrange("p u d -> p d u"),
             )
 
         def quantise_f(b):
             nc.vector.quantize_mx(
                 out=f_codes[:, b].rearrange("p g d -> p (g d)").bitcast(FP8X4),
                 scales=f_scales[:, b].rearrange("p g d -> p (g d)"),
-                in_=f_grouped[:, b].rearrange("p g d t -> p (g d t)"),
+                in_=f_grouped[:, b].rearrange("p g m -> p (g m)"),
             )
 
         rowmax = keep.tile([P, 1], F32)
@@ -151,14 +161,14 @@ def tile_image_aggregation_pa_s_kernel(tc, h_cluster, w2c, b2c, scores, temperat
         d_cols_ps = {}
         for g in range(PASSES):
             nc.vector.tensor_scalar(
-                out=d_rows[:, pass_pixels(g)],
-                in0=s_rows[:, pass_pixels(g)],
+                out=d_rows[:, pass_pixels(g)].rearrange("p (u e q) -> p u e q", u=2, e=2),
+                in0=s_rows[:, pass_pixels(g)].rearrange("p (u q e) -> p u e q", u=2, e=2),
                 scalar1=rowmax[:, 0:1],
                 scalar2=-1.0,
                 op0=ALU.subtract,
                 op1=ALU.mult,
             )
-            d_cols_ps[g] = stay.tile([P, PACK, BK], F32, name="d_cols_ps%d" % g)
+            d_cols_ps[g] = banks.tile([P, PACK, BK], F32, tag="bank", name="d_cols_ps%d" % g)
             for t in range(PACK):
                 nc.tensor.transpose(d_cols_ps[g][:, t, :], d_rows[:, chunk_pixels(g * PACK + t)], ident[:])
 
@@ -168,9 +178,6 @@ def tile_image_aggregation_pa_s_kernel(tc, h_cluster, w2c, b2c, scores, temperat
 
         w_words = w_rows[:].bitcast(F32).rearrange("d (p u) -> d u p", u=2)
         w_ps = banks.tile([P, 2, D], F32, tag="bank")
-        spread_ps = vecs.tile([P, D + 2], F32, tag="vec")
-        nc.tensor.matmul(out=spread_ps[:], lhsT=ones_bf[:], rhs=row_bf[:], start=True, stop=True)
-        bias_rows = keep.tile([P, D], F32)
         for u in range(2):
             nc.tensor.transpose(w_ps[:, u, :], w_words[:, u, :], ident[:])
 
@@ -192,7 +199,9 @@ def tile_image_aggregation_pa_s_kernel(tc, h_cluster, w2c, b2c, scores, temperat
                         bias=colmin[:, g * PACK + t, b : b + 1],
                     )
 
-        nc.scalar.copy(out=bias_rows[:], in_=spread_ps[:, 0:D])
+        nc.scalar.copy(
+            out=w_grouped[:].bitcast(F32).rearrange("p (d u) -> p d u", u=2), in_=w_ps[:].rearrange("p u d -> p d u")
+        )
 
         a_col = keep.tile([P, 1], F32)
         a_own = keep.tile([P, B], F32)
@@ -200,22 +209,58 @@ def tile_image_aggregation_pa_s_kernel(tc, h_cluster, w2c, b2c, scores, temperat
         nc.vector.reciprocal(out=a_col[:], in_=first_sum[:])
         nc.vector.tensor_scalar(out=a_pair[:, HI, :], in0=own_image[:], scalar1=a_col[:, 0:1], scalar2=None, op0=ALU.mult)
         nc.vector.tensor_scalar(out=a_own[:], in0=own_image[:], scalar1=a_col[:, 0:1], scalar2=None, op0=ALU.mult)
-        nc.vector.tensor_tensor(out=a_pair[:, LO, :], in0=a_own[:], in1=a_pair[:, HI, :], op=ALU.subtract)
-
-        for g in range(PASSES):
-            chunks = pass_chunks(g)
+        def make_high(k):
+            chunks = slice(2 * k, 2 * k + 2)
             nc.vector.tensor_copy(out=g_cols_pair[:, HI, chunks, :], in_=g_cols[:, chunks, :])
+
+        def make_low(k):
+            chunks = slice(2 * k, 2 * k + 2)
             nc.vector.tensor_tensor(
                 out=g_cols_pair[:, LO, chunks, :],
                 in0=g_cols[:, chunks, :],
                 in1=g_cols_pair[:, HI, chunks, :],
                 op=ALU.subtract,
             )
-            pair_ps = banks.tile([P, 2, PACK, P], BF16, tag="bank")
-            for part in (HI, LO):
-                for t in range(PACK):
-                    nc.tensor.transpose(pair_ps[:, part, t, :], g_cols_pair[:, part, g * PACK + t, :], ident_bf[:])
-            nc.scalar.copy(out=g_rows_pair[:, :, pass_pixels(g)], in_=pair_ps[:].rearrange("p i t n -> p i (t n)"))
+
+        def turn(ps, at, part, k):
+            for t in range(2):
+                nc.tensor.transpose(ps[:, (at + t) * P : (at + t + 1) * P], g_cols_pair[:, part, 2 * k + t, :], ident_bf[:])
+
+        def bank_of_pairs(name):
+            return banks.tile([P, 6 * P], BF16, tag="bank", name=name)
+
+        def take(ps, at, part, k, quarters):
+            width = quarters * 2 * P
+            nc.scalar.copy(
+                out=g_rows_pair[:, part, k * 2 * P : k * 2 * P + width], in_=ps[:, at * P : at * P + width]
+            )
+
+        make_high(0)
+        nc.vector.tensor_tensor(out=a_pair[:, LO, :], in0=a_own[:], in1=a_pair[:, HI, :], op=ALU.subtract)
+        make_low(0)
+        make_high(1)
+        make_high(2)
+        make_low(1)
+        make_high(3)
+        make_low(2)
+        make_low(3)
+        ps = bank_of_pairs("pairs0")
+        turn(ps, 0, HI, 0)
+        turn(ps, 2, LO, 0)
+        take(ps, 0, HI, 0, 1)
+        take(ps, 2, LO, 0, 1)
+        ps = bank_of_pairs("pairs1")
+        turn(ps, 0, HI, 1)
+        turn(ps, 2, HI, 2)
+        turn(ps, 4, LO, 1)
+        take(ps, 0, HI, 1, 2)
+        take(ps, 4, LO, 1, 1)
+        ps = bank_of_pairs("pairs2")
+        turn(ps, 0, HI, 3)
+        turn(ps, 2, LO, 2)
+        turn(ps, 4, LO, 3)
+        take(ps, 0, HI, 3, 1)
+        take(ps, 2, LO, 2, 2)
 
         PRODUCTS = ((LO, HI), (HI, HI), (HI, LO))
         ctx.enter_context(nc.allow_low_precision("v[HI] is v rounded to bfloat16; v[LO] holds what that leaves"))
@@ -225,138 +270,168 @@ def tile_image_aggregation_pa_s_kernel(tc, h_cluster, w2c, b2c, scores, temperat
             nc.vector.reciprocal(out=value, in_=sums)
             nc.vector.tensor_tensor(out=lo, in0=value, in1=hi, op=ALU.subtract)
 
-        nc.vector.tensor_copy(
-            out=w_grouped[:].bitcast(F32).rearrange("p (d u) -> p d u", u=2), in_=w_ps[:].rearrange("p u d -> p d u")
-        )
         inv_temp = keep.tile([P, 1], F32)
         neg_inv_temp = keep.tile([P, 1], F32)
-        nc.vector.reciprocal(out=inv_temp[:], in_=spread_ps[:, D : D + 1])
+        bias_col = keep.tile([P, 2], F32)
         regroup_h(0, nc.vector.tensor_copy)
+        nc.vector.quantize_mx(out=w_codes[:].bitcast(FP8X4), scales=w_scales[:], in_=w_grouped[:])
+        quantise_h(0)
+        regroup_h(1, nc.vector.tensor_copy)
+        regroup_h(2, nc.scalar.copy)
+
+        b_vec = keep.tile([P, CHUNKS, B], F32)
+        b_pair = keep.tile([P, 2, CHUNKS, B], BF16)
+        z_ps = {}
+        y_ps = {}
+
+        def sum_over_clusters(r, by_half=False):
+            z_ps[r] = vecs.tile([P, CHUNKS, B], F32, tag="vec", name="z_ps%d" % r)
+            order = [(i, c) for i in range(len(PRODUCTS)) for c in range(CHUNKS)]
+            if by_half:
+                order.sort(key=lambda ic: ic[1] // 2)
+            for i, c in order:
+                g_part, v_part = PRODUCTS[i]
+                nc.tensor.matmul(
+                    out=z_ps[r][:, c, :],
+                    lhsT=g_rows_pair[:, g_part, chunk_pixels(c)],
+                    rhs=a_pair[:, v_part, :],
+                    start=((i, c) == order[0]),
+                    stop=((i, c) == order[-1]),
+                )
+
+        def make_b(r):
+            reciprocal_pair(b_pair[:, HI], b_pair[:, LO], b_vec[:], z_ps[r][:])
+
+        def sum_over_pixels(r):
+            y_ps[r] = vecs.tile([P, B], F32, tag="vec", name="y_ps%d" % r)
+            nc.tensor.matmul(out=y_ps[r][:], lhsT=ident_bf[:], rhs=other_image[:], start=True, stop=False)
+            for i, (g_part, v_part) in enumerate(PRODUCTS):
+                for c in range(CHUNKS):
+                    nc.tensor.matmul(
+                        out=y_ps[r][:],
+                        lhsT=g_cols_pair[:, g_part, c, :],
+                        rhs=b_pair[:, v_part, c, :],
+                        start=False,
+                        stop=(i == len(PRODUCTS) - 1 and c == CHUNKS - 1),
+                    )
+
+        def make_a(r):
+            reciprocal_pair(a_pair[:, HI], a_pair[:, LO], a_own[:], y_ps[r][:])
+
+        sum_over_clusters(0, by_half=True)
+        spread_ps = vecs.tile([P, 2, 2], F32, tag="vec")
+        nc.tensor.matmul(out=spread_ps[:, 0, :], lhsT=ones_bf[:], rhs=row_bf[:, D : D + 2], start=True, stop=True)
+        nc.tensor.matmul(out=spread_ps[:, 1, :], lhsT=row_bf[:, 0:D], rhs=ones_bf[:, 0:2], start=True, stop=True)
+        multiply_f(0)
+        make_b(0)
+        nc.vector.tensor_copy(out=bias_col[:], in_=spread_ps[:, 1, :])
+        nc.vector.reciprocal(out=inv_temp[:], in_=spread_ps[:, 0, 0:1])
+        add_bias(0)
+        quantise_h(1)
         nc.vector.tensor_scalar_mul(out=neg_inv_temp[:], in0=inv_temp[:], scalar1=-1.0)
         nc.vector.tensor_scalar_mul(
             out=colmin_t[:].rearrange("p c b -> p (c b)"),
             in0=colmin[:].rearrange("p c b -> p (c b)"),
             scalar1=inv_temp[:, 0:1],
         )
-        nc.vector.quantize_mx(out=w_codes[:].bitcast(FP8X4), scales=w_scales[:], in_=w_grouped[:])
-        regroup_h(1, nc.vector.tensor_copy)
-        quantise_h(0)
-        regroup_h(2, nc.scalar.copy)
-        regroup_h(3, nc.scalar.copy)
-
-        def ride_along_tensor(s):
-            if s < PIECES:
-                multiply_f(s)
-
-        def ride_along_vector(s):
-            if s + 1 < PIECES:
-                quantise_h(s + 1)
-            if s < PIECES:
-                add_bias(s)
-            if s == PIECES - 1:
-                quantise_f(0)
-
-        b_vec = keep.tile([P, CHUNKS, B], F32)
-        b_pair = keep.tile([P, 2, CHUNKS, B], BF16)
+        regroup_h(3, nc.vector.tensor_copy)
+        sum_over_pixels(0)
+        multiply_f(1)
+        turn_f(0)
+        add_bias(1)
+        make_a(0)
+        quantise_h(2)
+        group_f(0, nc.vector.tensor_copy)
+        sum_over_clusters(1)
+        multiply_f(2)
+        turn_f(1)
+        table_ready = keep.tile([P, 1], F32)
+        nc.scalar.activation(out=table_ready[:], in_=inv_temp[:], func=ACT.Ln)
+        add_bias(2)
+        make_b(1)
+        quantise_h(3)
+        group_f(1, nc.vector.tensor_copy)
+        sum_over_pixels(1)
+        multiply_f(3)
+        make_a(1)
+        nc.vector.reduce_sum(out=a_col[:], in_=a_own[:], axis=AXIS_X)
         ln_a_col = keep.tile([P, 1], F32)
+        nc.scalar.activation(out=ln_a_col[:], in_=a_col[:], func=ACT.Ln)
+        add_bias(3)
+        log_ga = keep.tile([P, N], F32)
+        log_ga_ps = {}
+        a_rows_ps = banks.tile([P, BK], F32, tag="bank")
+        sum_over_clusters(2)
+        nc.tensor.transpose(a_rows_ps[:], a_col[:, 0:1].to_broadcast([P, P]), ident[:])
+        for g in range(PASSES):
+            nc.vector.tensor_scalar(
+                out=log_ga[:, pass_pixels(g)],
+                in0=d_rows[:, pass_pixels(g)],
+                scalar1=-1.0,
+                scalar2=ln_a_col[:, 0:1],
+                op0=ALU.mult,
+                op1=ALU.add,
+            )
+            log_ga_ps[g] = banks.tile([P, PACK, BK], F32, tag="bank", name="log_ga_ps%d" % g)
+            for t in range(PACK):
+                nc.tensor.transpose(log_ga_ps[g][:, t, :], log_ga[:, chunk_pixels(g * PACK + t)], ident[:])
+        turn_f(2)
+        turn_f(3)
         ga = keep.tile([P, CHUNKS, BK], F32)
-        ln_a_rows = keep.tile([P, BK], F32)
-        a_rows_ps = None
-        ln_a_rows_ps = None
-        z_ps = None
-        for r in range(ROUNDS):
-            last = r == ROUNDS - 1
-            z_ps = vecs.tile([P, CHUNKS, B], F32, tag="vec")
-            order = [(i, c) for i in range(len(PRODUCTS)) for c in range(CHUNKS)]
-            if r == 0:
-                order.sort(key=lambda ic: ic[1] // PACK)
-            for i, c in order:
-                g_part, v_part = PRODUCTS[i]
-                if last and (i, c) == (1, 0):
-                    a_rows_ps = vecs.tile([P, BK], F32, tag="vec")
-                    nc.tensor.transpose(a_rows_ps[:], a_col[:, 0:1].to_broadcast([P, P]), ident[:])
-                if last and (i, c) == (2, 0):
-                    ln_a_rows_ps = vecs.tile([P, BK], F32, tag="vec")
-                    nc.tensor.transpose(ln_a_rows_ps[:], ln_a_col[:, 0:1].to_broadcast([P, P]), ident[:])
-                nc.tensor.matmul(
-                    out=z_ps[:, c, :],
-                    lhsT=g_rows_pair[:, g_part, chunk_pixels(c)],
-                    rhs=a_pair[:, v_part, :],
-                    start=((i, c) == order[0]),
-                    stop=((i, c) == order[-1]),
-                )
-            ride_along_tensor(2 * r)
-            if last:
-                nc.scalar.copy(out=ln_a_rows[:], in_=ln_a_rows_ps[:])
-                nc.vector.tensor_tensor(
-                    out=ga[:], in0=g_cols[:], in1=a_rows_ps[:].unsqueeze(1).to_broadcast([P, CHUNKS, BK]), op=ALU.mult
-                )
-                quantise_f(1)
-            else:
-                reciprocal_pair(b_pair[:, HI], b_pair[:, LO], b_vec[:], z_ps[:])
-                ride_along_vector(2 * r)
-
-                y_ps = vecs.tile([P, B], F32, tag="vec")
-                nc.tensor.matmul(out=y_ps[:], lhsT=ident_bf[:], rhs=other_image[:], start=True, stop=False)
-                for i, (g_part, v_part) in enumerate(PRODUCTS):
-                    for c in range(CHUNKS):
-                        nc.tensor.matmul(
-                            out=y_ps[:],
-                            lhsT=g_cols_pair[:, g_part, c, :],
-                            rhs=b_pair[:, v_part, c, :],
-                            start=False,
-                            stop=(i == len(PRODUCTS) - 1 and c == CHUNKS - 1),
-                        )
-                ride_along_tensor(2 * r + 1)
-                reciprocal_pair(a_pair[:, HI], a_pair[:, LO], a_own[:], y_ps[:])
-                if r == ROUNDS - 2:
-                    nc.vector.reduce_sum(out=a_col[:], in_=a_own[:], axis=AXIS_X)
-                    nc.scalar.activation(out=ln_a_col[:], in_=a_col[:], func=ACT.Ln)
-                ride_along_vector(2 * r + 1)
+        nc.vector.tensor_tensor(
+            out=ga[:, 0:PRODUCT_CHUNKS, :],
+            in0=g_cols[:, 0:PRODUCT_CHUNKS, :],
+            in1=a_rows_ps[:].unsqueeze(1).to_broadcast([P, PRODUCT_CHUNKS, BK]),
+            op=ALU.mult,
+        )
 
         ln_z = keep.tile([P, CHUNKS, B], F32)
-        nc.scalar.activation(out=ln_z[:], in_=z_ps[:], func=ACT.Ln)
-        nc.vector.reciprocal(out=b_vec[:], in_=z_ps[:])
-        log_ga = keep.tile([P, CHUNKS, BK], F32)
+        nc.scalar.activation(out=ln_z[:], in_=z_ps[ROUNDS - 1][:], func=ACT.Ln)
         ln_beta = keep.tile([P, CHUNKS, B], F32)
         plain = keep.tile([P, CHUNKS, BK], F32)
         tempered = keep.tile([P, CHUNKS, BK], F32)
-        for g in range(PASSES):
-            chunks = pass_chunks(g)
-            nc.vector.tensor_tensor(
-                out=log_ga[:, chunks, :],
-                in0=ln_a_rows[:].unsqueeze(1).to_broadcast([P, PACK, BK]),
-                in1=d_cols_ps[g][:],
-                op=ALU.subtract,
-            )
-            if g == 0:
-                nc.vector.scalar_tensor_tensor(
-                    out=ln_beta[:].rearrange("p c b -> p (c b)"),
-                    in0=ln_z[:].rearrange("p c b -> p (c b)"),
-                    scalar=neg_inv_temp[:, 0:1],
-                    in1=colmin_t[:].rearrange("p c b -> p (c b)"),
-                    op0=ALU.mult,
-                    op1=ALU.add,
-                )
+        nc.vector.scalar_tensor_tensor(
+            out=ln_beta[:].rearrange("p c b -> p (c b)"),
+            in0=ln_z[:].rearrange("p c b -> p (c b)"),
+            scalar=neg_inv_temp[:, 0:1],
+            in1=colmin_t[:].rearrange("p c b -> p (c b)"),
+            op0=ALU.mult,
+            op1=ALU.add,
+        )
+        nc.vector.reciprocal(out=b_vec[:], in_=z_ps[ROUNDS - 1][:])
+        ln_b = keep.tile([P, CHUNKS, B], F32)
+        nc.vector.scalar_tensor_tensor(
+            out=ln_b[:], in0=ln_z[:], scalar=-1.0, in1=colmin[:], op0=ALU.mult, op1=ALU.add
+        )
         for c in range(CHUNKS):
             for b in range(B):
                 nc.scalar.activation(
                     out=tempered[:, c, image_clusters(b)],
-                    in_=log_ga[:, c, image_clusters(b)],
+                    in_=log_ga_ps[c // PACK][:, c % PACK, image_clusters(b)],
                     func=ACT.Exp,
                     scale=inv_temp[:, 0:1],
                     bias=ln_beta[:, c, b : b + 1],
                 )
-        table_ready = keep.tile([P, 1], F32)
+        for c in range(PRODUCT_CHUNKS, CHUNKS):
+            for b in range(B):
+                nc.scalar.activation(
+                    out=plain[:, c, image_clusters(b)],
+                    in_=log_ga_ps[c // PACK][:, c % PACK, image_clusters(b)],
+                    func=ACT.Exp,
+                    bias=ln_b[:, c, b : b + 1],
+                )
         nc.scalar.activation(out=table_ready[:], in_=inv_temp[:], func=ACT.Abs_reciprocal_sqrt)
-        for g in range(PASSES):
-            chunks = pass_chunks(g)
+        for chunks in (slice(0, PACK), slice(PACK, PRODUCT_CHUNKS)):
             nc.vector.tensor_tensor(
                 out=by_image(plain[:, chunks, :]),
                 in0=by_image(ga[:, chunks, :]),
-                in1=b_vec[:, chunks, :].unsqueeze(3).to_broadcast([P, PACK, B, K]),
+                in1=b_vec[:, chunks, :].unsqueeze(3).to_broadcast([P, chunks.stop - chunks.start, B, K]),
                 op=ALU.mult,
             )
+        group_f(2, nc.vector.tensor_copy)
+        group_f(3, nc.vector.tensor_copy)
+        for b in range(B):
+            quantise_f(b)
 
         p_grouped = keep.tile([P, PASSES, BK, PACK], BF16, align_bytes=64)
         p_codes = keep.tile([P, PASSES, BK], U32, align_bytes=64)

@@ -156,7 +156,10 @@ def tile_image_aggregation_pa_s_kernel(tc, h_cluster, w2c, b2c, scores, temperat
             )
 
         rowmax = keep.tile([P, 1], F32)
-        nc.vector.reduce_max(out=rowmax[:], in_=s_rows[:], axis=AXIS_X)
+        s_again = keep.tile([P, N], BF16)
+        nc.vector.tensor_scalar(
+            out=s_again[:], in0=s_rows[:], scalar1=1.0, scalar2=None, op0=ALU.mult, op1=ALU.max, accum_out=rowmax[:]
+        )
         d_rows = keep.tile([P, N], F32)
         d_cols_ps = {}
         for g in range(PASSES):
@@ -373,10 +376,9 @@ def tile_image_aggregation_pa_s_kernel(tc, h_cluster, w2c, b2c, scores, temperat
                 op1=ALU.add,
             )
             log_ga_ps[g] = banks.tile([P, PACK, BK], F32, tag="bank", name="log_ga_ps%d" % g)
+            turn_f(2 + g)
             for t in range(PACK):
                 nc.tensor.transpose(log_ga_ps[g][:, t, :], log_ga[:, chunk_pixels(g * PACK + t)], ident[:])
-        turn_f(2)
-        turn_f(3)
         ga = keep.tile([P, CHUNKS, BK], F32)
         nc.vector.tensor_tensor(
             out=ga[:, 0:PRODUCT_CHUNKS, :],
@@ -387,6 +389,7 @@ def tile_image_aggregation_pa_s_kernel(tc, h_cluster, w2c, b2c, scores, temperat
 
         ln_z = keep.tile([P, CHUNKS, B], F32)
         nc.scalar.activation(out=ln_z[:], in_=z_ps[ROUNDS - 1][:], func=ACT.Ln)
+        nc.scalar.activation(out=table_ready[:], in_=inv_temp[:], func=ACT.Exp)
         ln_beta = keep.tile([P, CHUNKS, B], F32)
         plain = keep.tile([P, CHUNKS, BK], F32)
         tempered = keep.tile([P, CHUNKS, BK], F32)
@@ -403,23 +406,23 @@ def tile_image_aggregation_pa_s_kernel(tc, h_cluster, w2c, b2c, scores, temperat
         nc.vector.scalar_tensor_tensor(
             out=ln_b[:], in0=ln_z[:], scalar=-1.0, in1=colmin[:], op0=ALU.mult, op1=ALU.add
         )
-        for c in range(CHUNKS):
+        for g in range(PASSES):
             for b in range(B):
-                nc.scalar.activation(
-                    out=tempered[:, c, image_clusters(b)],
-                    in_=log_ga_ps[c // PACK][:, c % PACK, image_clusters(b)],
-                    func=ACT.Exp,
-                    scale=inv_temp[:, 0:1],
-                    bias=ln_beta[:, c, b : b + 1],
-                )
-        for c in range(PRODUCT_CHUNKS, CHUNKS):
-            for b in range(B):
-                nc.scalar.activation(
-                    out=plain[:, c, image_clusters(b)],
-                    in_=log_ga_ps[c // PACK][:, c % PACK, image_clusters(b)],
-                    func=ACT.Exp,
-                    bias=ln_b[:, c, b : b + 1],
-                )
+                for c in range(g * PACK, (g + 1) * PACK):
+                    nc.scalar.activation(
+                        out=tempered[:, c, image_clusters(b)],
+                        in_=log_ga_ps[g][:, c % PACK, image_clusters(b)],
+                        func=ACT.Exp,
+                        scale=inv_temp[:, 0:1],
+                        bias=ln_beta[:, c, b : b + 1],
+                    )
+                for c in range(max(PRODUCT_CHUNKS, g * PACK), (g + 1) * PACK):
+                    nc.scalar.activation(
+                        out=plain[:, c, image_clusters(b)],
+                        in_=log_ga_ps[g][:, c % PACK, image_clusters(b)],
+                        func=ACT.Exp,
+                        bias=ln_b[:, c, b : b + 1],
+                    )
         nc.scalar.activation(out=table_ready[:], in_=inv_temp[:], func=ACT.Abs_reciprocal_sqrt)
         for chunks in (slice(0, PACK), slice(PACK, PRODUCT_CHUNKS)):
             nc.vector.tensor_tensor(
@@ -441,12 +444,14 @@ def tile_image_aggregation_pa_s_kernel(tc, h_cluster, w2c, b2c, scores, temperat
             agg_ps[b] = banks.tile([P, BK], F32, tag="bank", name="agg_ps%d" % b)
         for g in range(PASSES):
             chunks = pass_chunks(g)
-            nc.vector.tensor_tensor(
-                out=p_grouped[:, g],
-                in0=plain[:, chunks, :].rearrange("p t m -> p m t"),
-                in1=tempered[:, chunks, :].rearrange("p t m -> p m t"),
-                op=ALU.add,
-            )
+            for b in range(B):
+                own = image_clusters(b)
+                nc.vector.tensor_tensor(
+                    out=p_grouped[:, g, own, :],
+                    in0=plain[:, chunks, own].rearrange("p t m -> p m t"),
+                    in1=tempered[:, chunks, own].rearrange("p t m -> p m t"),
+                    op=ALU.add,
+                )
             nc.vector.quantize_mx(
                 out=p_codes[:, g, :].bitcast(FP8X4),
                 scales=p_scales[:, g, :],

@@ -82,13 +82,9 @@ def tile_image_aggregation_pa_s_kernel(tc, h_cluster, w2c, b2c, scores, temperat
         nc.scalar.dma_start(out=row_bf[0:1, D : D + 1], in_=temperature.unsqueeze(0))
         w_rows = keep.tile([P, HID], BF16)
         nc.sync.dma_start(out=w_rows[:], in_=w2c)
-        h_raw = keep.tile([P, PIECES, PACK, P * PACK], BF16)
-        for q in range(PIECES):
-            b, g = q % B, q // B
-            nc.sync.dma_start(
-                out=h_raw[:, q],
-                in_=h_cluster[b].rearrange("(p j) n -> p j n", j=PACK)[:, :, pass_pixels(g)],
-            )
+        h_raw = keep.tile([P, B, PACK, N], BF16)
+        for b in range(B):
+            nc.sync.dma_start(out=h_raw[:, b], in_=h_cluster[b].rearrange("(p j) n -> p j n", j=PACK))
 
         w_grouped = keep.tile([P, D * PACK], BF16, align_bytes=64)
         w_codes = keep.tile([P, D], U32, align_bytes=64)
@@ -104,14 +100,14 @@ def tile_image_aggregation_pa_s_kernel(tc, h_cluster, w2c, b2c, scores, temperat
         f_turned_ps = {}
 
         def regroup_h(q, copy):
-            b, g = q % B, q // B
+            b, g = q // PASSES, q % PASSES
             copy(
                 out=h_grouped[:, b, pass_pixels(g), :].rearrange("p (c i) j -> p c j i", i=RUN),
-                in_=h_raw[:, q].rearrange("p j (c i) -> p c j i", i=RUN),
+                in_=h_raw[:, b, :, pass_pixels(g)].rearrange("p j (c i) -> p c j i", i=RUN),
             )
 
         def quantise_h(q):
-            b, g = q % B, q // B
+            b, g = q // PASSES, q % PASSES
             nc.vector.quantize_mx(
                 out=h_codes[:, b, pass_pixels(g)].bitcast(FP8X4),
                 scales=h_scales[:, b, pass_pixels(g)],
@@ -119,7 +115,7 @@ def tile_image_aggregation_pa_s_kernel(tc, h_cluster, w2c, b2c, scores, temperat
             )
 
         def multiply_f(q):
-            b, g = q % B, q // B
+            b, g = q // PASSES, q % PASSES
             f_ps[q] = banks.tile([P, P * PACK], F32, tag="bank", name="f_ps%d" % q)
             for repeat in range(DUMMIES[q] + 1):
               nc.tensor.matmul_mx(
@@ -142,7 +138,7 @@ def tile_image_aggregation_pa_s_kernel(tc, h_cluster, w2c, b2c, scores, temperat
                 nc.tensor.transpose(f_turned_ps[q][:, u, :], words[:, u * P : (u + 1) * P], ident[:])
 
         def group_f(q, copy):
-            b, g = q % B, q // B
+            b, g = q // PASSES, q % PASSES
             copy(
                 out=f_grouped[:, b, g].bitcast(F32).rearrange("p (d u) -> p d u", u=2),
                 in_=f_turned_ps[q][:].rearrange("p u d -> p d u"),
@@ -171,9 +167,10 @@ def tile_image_aggregation_pa_s_kernel(tc, h_cluster, w2c, b2c, scores, temperat
                 op0=ALU.subtract,
                 op1=ALU.mult,
             )
-            d_cols_ps[g] = banks.tile([P, PACK, BK], F32, tag="bank", name="d_cols_ps%d" % g)
-            for t in range(PACK):
-                nc.tensor.transpose(d_cols_ps[g][:, t, :], d_rows[:, chunk_pixels(g * PACK + t)], ident[:])
+            for k in range(2 * g, 2 * g + 2):
+                d_cols_ps[k] = banks.tile([P, 2, BK], F32, tag="bank", name="d_cols_ps%d" % k)
+                for t in range(2):
+                    nc.tensor.transpose(d_cols_ps[k][:, t, :], d_rows[:, chunk_pixels(2 * k + t)], ident[:])
 
         exp_rows = keep.tile([P, N], BF16)
         first_sum = keep.tile([P, 1], F32)
@@ -189,19 +186,19 @@ def tile_image_aggregation_pa_s_kernel(tc, h_cluster, w2c, b2c, scores, temperat
         g_cols = keep.tile([P, CHUNKS, BK], F32)
         g_cols_pair = keep.tile([P, 2, CHUNKS, BK], BF16)
         g_rows_pair = keep.tile([P, 2, N], BF16)
-        for g in range(PASSES):
-            chunks = pass_chunks(g)
-            nc.vector.tensor_reduce(out=colmin[:, chunks, :], in_=by_image(d_cols_ps[g][:]), axis=AXIS_X, op=ALU.min)
-            for t in range(PACK):
+        for k in range(CHUNKS // 2):
+            nc.vector.tensor_reduce(
+                out=colmin[:, 2 * k : 2 * k + 2, :], in_=by_image(d_cols_ps[k][:]), axis=AXIS_X, op=ALU.min
+            )
+            for t in range(2):
                 for b in range(B):
                     nc.scalar.activation(
-                        out=g_cols[:, g * PACK + t, image_clusters(b)],
-                        in_=d_cols_ps[g][:, t, image_clusters(b)],
+                        out=g_cols[:, 2 * k + t, image_clusters(b)],
+                        in_=d_cols_ps[k][:, t, image_clusters(b)],
                         func=ACT.Exp,
                         scale=-1.0,
-                        bias=colmin[:, g * PACK + t, b : b + 1],
+                        bias=colmin[:, 2 * k + t, b : b + 1],
                     )
-
         nc.scalar.copy(
             out=w_grouped[:].bitcast(F32).rearrange("p (d u) -> p d u", u=2), in_=w_ps[:].rearrange("p u d -> p d u")
         )
@@ -358,6 +355,7 @@ def tile_image_aggregation_pa_s_kernel(tc, h_cluster, w2c, b2c, scores, temperat
         multiply_f(3)
         make_a(1)
         nc.vector.reduce_sum(out=a_col[:], in_=a_own[:], axis=AXIS_X)
+        quantise_f(0)
         ln_a_col = keep.tile([P, 1], F32)
         nc.scalar.activation(out=ln_a_col[:], in_=a_col[:], func=ACT.Ln)
         add_bias(3)
@@ -433,8 +431,7 @@ def tile_image_aggregation_pa_s_kernel(tc, h_cluster, w2c, b2c, scores, temperat
             )
         group_f(2, nc.vector.tensor_copy)
         group_f(3, nc.vector.tensor_copy)
-        for b in range(B):
-            quantise_f(b)
+        quantise_f(1)
 
         p_grouped = keep.tile([P, PASSES, BK, PACK], BF16, align_bytes=64)
         p_codes = keep.tile([P, PASSES, BK], U32, align_bytes=64)

@@ -24,7 +24,7 @@ HI, LO = 0, 1
 FAR = 2.0**120
 RUN = 4
 
-DUMMIES = (1, 1, 1, 0)
+KEEP = (12, 3, 3, 6, 3, 4, 4, 4, 4, 4)
 PRODUCT_CHUNKS = 6
 FLOPS = 2 * B * (D * HID * N + D * K * N)
 
@@ -54,7 +54,8 @@ def tile_image_aggregation_pa_s_kernel(tc, h_cluster, w2c, b2c, scores, temperat
     with ExitStack() as ctx:
         ctx.enter_context(tc.manual_schedule())
         keep = ctx.enter_context(tc.tile_pool(name="keep", bufs=1))
-        banks = ctx.enter_context(tc.psum_pool(name="banks", bufs=5))
+        banks = ctx.enter_context(tc.psum_pool(name="banks", bufs=4))
+        spare = ctx.enter_context(tc.psum_pool(name="spare", bufs=1))
         vecs = ctx.enter_context(tc.psum_pool(name="vecs", bufs=3))
 
         row_bf = keep.tile([P, D + 2], BF16)
@@ -99,6 +100,20 @@ def tile_image_aggregation_pa_s_kernel(tc, h_cluster, w2c, b2c, scores, temperat
         f_ps = {}
         f_turned_ps = {}
 
+        spare_ps = spare.tile([P, D], F32)
+
+        def keep_clock(passes):
+            for i in range(passes):
+                nc.tensor.matmul_mx(
+                    out=spare_ps[:],
+                    lhsT=w_codes[:].bitcast(FP8X4),
+                    lhsT_scale=w_scales[:],
+                    rhs=w_codes[:].bitcast(FP8X4),
+                    rhs_scale=w_scales[:],
+                    start=True,
+                    stop=True,
+                )
+
         def regroup_h(q, copy):
             b, g = q // PASSES, q % PASSES
             copy(
@@ -117,8 +132,7 @@ def tile_image_aggregation_pa_s_kernel(tc, h_cluster, w2c, b2c, scores, temperat
         def multiply_f(q):
             b, g = q // PASSES, q % PASSES
             f_ps[q] = banks.tile([P, P * PACK], F32, tag="bank", name="f_ps%d" % q)
-            for repeat in range(DUMMIES[q] + 1):
-              nc.tensor.matmul_mx(
+            nc.tensor.matmul_mx(
                 out=f_ps[q][:],
                 lhsT=w_codes[:].bitcast(FP8X4),
                 lhsT_scale=w_scales[:],
@@ -156,6 +170,10 @@ def tile_image_aggregation_pa_s_kernel(tc, h_cluster, w2c, b2c, scores, temperat
         nc.vector.tensor_scalar(
             out=s_again[:], in0=s_rows[:], scalar1=1.0, scalar2=None, op0=ALU.mult, op1=ALU.max, accum_out=rowmax[:]
         )
+        w_words = w_rows[:].bitcast(F32).rearrange("d (p u) -> d u p", u=2)
+        w_ps = banks.tile([P, 2, D], F32, tag="bank")
+        for u in range(2):
+            nc.tensor.transpose(w_ps[:, u, :], w_words[:, u, :], ident[:])
         d_rows = keep.tile([P, N], F32)
         d_cols_ps = {}
         for g in range(PASSES):
@@ -167,19 +185,17 @@ def tile_image_aggregation_pa_s_kernel(tc, h_cluster, w2c, b2c, scores, temperat
                 op0=ALU.subtract,
                 op1=ALU.mult,
             )
-            for k in range(2 * g, 2 * g + 2):
-                d_cols_ps[k] = banks.tile([P, 2, BK], F32, tag="bank", name="d_cols_ps%d" % k)
-                for t in range(2):
-                    nc.tensor.transpose(d_cols_ps[k][:, t, :], d_rows[:, chunk_pixels(2 * k + t)], ident[:])
+        nc.vector.tensor_copy(
+            out=w_grouped[:].bitcast(F32).rearrange("p (d u) -> p d u", u=2), in_=w_ps[:].rearrange("p u d -> p d u")
+        )
+        for k in range(CHUNKS // 2):
+            d_cols_ps[k] = banks.tile([P, 2, BK], F32, tag="bank", name="d_cols_ps%d" % k)
+            for t in range(2):
+                nc.tensor.transpose(d_cols_ps[k][:, t, :], d_rows[:, chunk_pixels(2 * k + t)], ident[:])
 
         exp_rows = keep.tile([P, N], BF16)
         first_sum = keep.tile([P, 1], F32)
         nc.scalar.activation(out=exp_rows[:], in_=d_rows[:], func=ACT.Exp, scale=-1.0, accum_out=first_sum[:])
-
-        w_words = w_rows[:].bitcast(F32).rearrange("d (p u) -> d u p", u=2)
-        w_ps = banks.tile([P, 2, D], F32, tag="bank")
-        for u in range(2):
-            nc.tensor.transpose(w_ps[:, u, :], w_words[:, u, :], ident[:])
 
         colmin = keep.tile([P, CHUNKS, B], F32)
         colmin_t = keep.tile([P, CHUNKS, B], F32)
@@ -190,6 +206,9 @@ def tile_image_aggregation_pa_s_kernel(tc, h_cluster, w2c, b2c, scores, temperat
             nc.vector.tensor_reduce(
                 out=colmin[:, 2 * k : 2 * k + 2, :], in_=by_image(d_cols_ps[k][:]), axis=AXIS_X, op=ALU.min
             )
+            if k == 0:
+                nc.vector.quantize_mx(out=w_codes[:].bitcast(FP8X4), scales=w_scales[:], in_=w_grouped[:])
+                keep_clock(KEEP[0])
             for t in range(2):
                 for b in range(B):
                     nc.scalar.activation(
@@ -199,10 +218,6 @@ def tile_image_aggregation_pa_s_kernel(tc, h_cluster, w2c, b2c, scores, temperat
                         scale=-1.0,
                         bias=colmin[:, 2 * k + t, b : b + 1],
                     )
-        nc.scalar.copy(
-            out=w_grouped[:].bitcast(F32).rearrange("p (d u) -> p d u", u=2), in_=w_ps[:].rearrange("p u d -> p d u")
-        )
-
         a_col = keep.tile([P, 1], F32)
         a_own = keep.tile([P, B], F32)
         a_pair = keep.tile([P, 2, B], BF16)
@@ -249,18 +264,21 @@ def tile_image_aggregation_pa_s_kernel(tc, h_cluster, w2c, b2c, scores, temperat
         turn(ps, 2, LO, 0)
         take(ps, 0, HI, 0, 1)
         take(ps, 2, LO, 0, 1)
+        keep_clock(KEEP[1])
         ps = bank_of_pairs("pairs1")
         turn(ps, 0, HI, 1)
         turn(ps, 2, HI, 2)
         turn(ps, 4, LO, 1)
         take(ps, 0, HI, 1, 2)
         take(ps, 4, LO, 1, 1)
+        keep_clock(KEEP[2])
         ps = bank_of_pairs("pairs2")
         turn(ps, 0, HI, 3)
         turn(ps, 2, LO, 2)
         turn(ps, 4, LO, 3)
         take(ps, 0, HI, 3, 1)
         take(ps, 2, LO, 2, 2)
+        keep_clock(KEEP[3])
 
         PRODUCTS = ((LO, HI), (HI, HI), (HI, LO))
         ctx.enter_context(nc.allow_low_precision("v[HI] is v rounded to bfloat16; v[LO] holds what that leaves"))
@@ -274,7 +292,6 @@ def tile_image_aggregation_pa_s_kernel(tc, h_cluster, w2c, b2c, scores, temperat
         neg_inv_temp = keep.tile([P, 1], F32)
         bias_col = keep.tile([P, 2], F32)
         regroup_h(0, nc.vector.tensor_copy)
-        nc.vector.quantize_mx(out=w_codes[:].bitcast(FP8X4), scales=w_scales[:], in_=w_grouped[:])
         quantise_h(0)
         regroup_h(1, nc.vector.tensor_copy)
         regroup_h(2, nc.scalar.copy)
@@ -298,6 +315,8 @@ def tile_image_aggregation_pa_s_kernel(tc, h_cluster, w2c, b2c, scores, temperat
                     start=((i, c) == order[0]),
                     stop=((i, c) == order[-1]),
                 )
+                if by_half and (i, c) in ((2, 1), (2, 3), (2, 5)):
+                    keep_clock(KEEP[4])
 
         def make_b(r):
             reciprocal_pair(b_pair[:, HI], b_pair[:, LO], b_vec[:], z_ps[r][:])
@@ -323,6 +342,7 @@ def tile_image_aggregation_pa_s_kernel(tc, h_cluster, w2c, b2c, scores, temperat
         nc.tensor.matmul(out=spread_ps[:, 0, :], lhsT=ones_bf[:], rhs=row_bf[:, D : D + 2], start=True, stop=True)
         nc.tensor.matmul(out=spread_ps[:, 1, :], lhsT=row_bf[:, 0:D], rhs=ones_bf[:, 0:2], start=True, stop=True)
         multiply_f(0)
+        keep_clock(KEEP[5])
         make_b(0)
         nc.vector.tensor_copy(out=bias_col[:], in_=spread_ps[:, 1, :])
         nc.vector.reciprocal(out=inv_temp[:], in_=spread_ps[:, 0, 0:1])
@@ -337,6 +357,7 @@ def tile_image_aggregation_pa_s_kernel(tc, h_cluster, w2c, b2c, scores, temperat
         regroup_h(3, nc.vector.tensor_copy)
         sum_over_pixels(0)
         multiply_f(1)
+        keep_clock(KEEP[6])
         turn_f(0)
         add_bias(1)
         make_a(0)
@@ -344,6 +365,7 @@ def tile_image_aggregation_pa_s_kernel(tc, h_cluster, w2c, b2c, scores, temperat
         group_f(0, nc.vector.tensor_copy)
         sum_over_clusters(1)
         multiply_f(2)
+        keep_clock(KEEP[7])
         turn_f(1)
         table_ready = keep.tile([P, 1], F32)
         nc.scalar.activation(out=table_ready[:], in_=inv_temp[:], func=ACT.Ln)
@@ -353,6 +375,7 @@ def tile_image_aggregation_pa_s_kernel(tc, h_cluster, w2c, b2c, scores, temperat
         group_f(1, nc.vector.tensor_copy)
         sum_over_pixels(1)
         multiply_f(3)
+        keep_clock(KEEP[8])
         make_a(1)
         nc.vector.reduce_sum(out=a_col[:], in_=a_own[:], axis=AXIS_X)
         quantise_f(0)
@@ -361,8 +384,9 @@ def tile_image_aggregation_pa_s_kernel(tc, h_cluster, w2c, b2c, scores, temperat
         add_bias(3)
         log_ga = keep.tile([P, N], F32)
         log_ga_ps = {}
-        a_rows_ps = banks.tile([P, BK], F32, tag="bank")
         sum_over_clusters(2)
+        keep_clock(KEEP[9])
+        a_rows_ps = vecs.tile([P, BK], F32, tag="vec")
         nc.tensor.transpose(a_rows_ps[:], a_col[:, 0:1].to_broadcast([P, P]), ident[:])
         for g in range(PASSES):
             nc.vector.tensor_scalar(

@@ -24,7 +24,7 @@ HI, LO = 0, 1
 FAR = 2.0**120
 RUN = 4
 
-KEEP = (12, 3, 3, 6, 3, 4, 4, 4, 4, 4)
+KEEP = (12, 3, 3, 6, 3, 4, 4, 4, 0, 2, 0)
 PRODUCT_CHUNKS = 6
 FLOPS = 2 * B * (D * HID * N + D * K * N)
 
@@ -114,11 +114,11 @@ def tile_image_aggregation_pa_s_kernel(tc, h_cluster, w2c, b2c, scores, temperat
                     stop=True,
                 )
 
-        def regroup_h(q, copy):
+        def regroup_h(q, copy, part=slice(0, P * PACK)):
             b, g = q // PASSES, q % PASSES
             copy(
-                out=h_grouped[:, b, pass_pixels(g), :].rearrange("p (c i) j -> p c j i", i=RUN),
-                in_=h_raw[:, b, :, pass_pixels(g)].rearrange("p j (c i) -> p c j i", i=RUN),
+                out=h_grouped[:, b, pass_pixels(g), :][:, part, :].rearrange("p (c i) j -> p c j i", i=RUN),
+                in_=h_raw[:, b, :, pass_pixels(g)][:, :, part].rearrange("p j (c i) -> p c j i", i=RUN),
             )
 
         def quantise_h(q):
@@ -143,7 +143,7 @@ def tile_image_aggregation_pa_s_kernel(tc, h_cluster, w2c, b2c, scores, temperat
             )
 
         def add_bias(q):
-            nc.scalar.activation(out=f_rows[:, q], in_=f_ps[q][:], func=ACT.Identity, bias=bias_col[:, 0:1])
+            nc.scalar.activation(out=f_rows[:, q], in_=f_ps[q][:], func=ACT.Identity, bias=spread[:, 1, 0:1])
 
         def turn_f(q):
             f_turned_ps[q] = banks.tile([P, 2, D], F32, tag="bank", name="f_turned_ps%d" % q)
@@ -165,10 +165,17 @@ def tile_image_aggregation_pa_s_kernel(tc, h_cluster, w2c, b2c, scores, temperat
                 in_=f_grouped[:, b].rearrange("p g m -> p (g m)"),
             )
 
-        rowmax = keep.tile([P, 1], F32)
-        s_again = keep.tile([P, N], BF16)
+        table_ready = keep.tile([P, 1], F32)
+        nc.scalar.activation(out=table_ready[:], in_=own_image[:, 0:1], func=ACT.Exp)
+        rowmin = keep.tile([P, 1], F32)
+        minus_s = keep.tile([P, N], BF16)
         nc.vector.tensor_scalar(
-            out=s_again[:], in0=s_rows[:], scalar1=1.0, scalar2=None, op0=ALU.mult, op1=ALU.max, accum_out=rowmax[:]
+            out=minus_s[:], in0=s_rows[:], scalar1=-1.0, scalar2=None, op0=ALU.mult, op1=ALU.min, accum_out=rowmin[:]
+        )
+        exp_rows = keep.tile([P, N], BF16)
+        first_sum = keep.tile([P, 1], F32)
+        nc.scalar.activation(
+            out=exp_rows[:], in_=s_rows[:], func=ACT.Exp, bias=rowmin[:, 0:1], accum_out=first_sum[:]
         )
         w_words = w_rows[:].bitcast(F32).rearrange("d (p u) -> d u p", u=2)
         w_ps = banks.tile([P, 2, D], F32, tag="bank")
@@ -176,14 +183,14 @@ def tile_image_aggregation_pa_s_kernel(tc, h_cluster, w2c, b2c, scores, temperat
             nc.tensor.transpose(w_ps[:, u, :], w_words[:, u, :], ident[:])
         d_rows = keep.tile([P, N], F32)
         d_cols_ps = {}
-        for g in range(PASSES):
+        for k in range(CHUNKS // 2):
+            quarter = slice(2 * k * P, (2 * k + 2) * P)
             nc.vector.tensor_scalar(
-                out=d_rows[:, pass_pixels(g)].rearrange("p (u e q) -> p u e q", u=2, e=2),
-                in0=s_rows[:, pass_pixels(g)].rearrange("p (u q e) -> p u e q", u=2, e=2),
-                scalar1=rowmax[:, 0:1],
-                scalar2=-1.0,
+                out=d_rows[:, quarter].rearrange("p (e q) -> p e q", e=2),
+                in0=minus_s[:, quarter].rearrange("p (q e) -> p e q", e=2),
+                scalar1=rowmin[:, 0:1],
+                scalar2=None,
                 op0=ALU.subtract,
-                op1=ALU.mult,
             )
         nc.vector.tensor_copy(
             out=w_grouped[:].bitcast(F32).rearrange("p (d u) -> p d u", u=2), in_=w_ps[:].rearrange("p u d -> p d u")
@@ -192,10 +199,6 @@ def tile_image_aggregation_pa_s_kernel(tc, h_cluster, w2c, b2c, scores, temperat
             d_cols_ps[k] = banks.tile([P, 2, BK], F32, tag="bank", name="d_cols_ps%d" % k)
             for t in range(2):
                 nc.tensor.transpose(d_cols_ps[k][:, t, :], d_rows[:, chunk_pixels(2 * k + t)], ident[:])
-
-        exp_rows = keep.tile([P, N], BF16)
-        first_sum = keep.tile([P, 1], F32)
-        nc.scalar.activation(out=exp_rows[:], in_=d_rows[:], func=ACT.Exp, scale=-1.0, accum_out=first_sum[:])
 
         colmin = keep.tile([P, CHUNKS, B], F32)
         colmin_t = keep.tile([P, CHUNKS, B], F32)
@@ -290,7 +293,7 @@ def tile_image_aggregation_pa_s_kernel(tc, h_cluster, w2c, b2c, scores, temperat
 
         inv_temp = keep.tile([P, 1], F32)
         neg_inv_temp = keep.tile([P, 1], F32)
-        bias_col = keep.tile([P, 2], F32)
+        spread = keep.tile([P, 2, 2], F32)
         regroup_h(0, nc.vector.tensor_copy)
         quantise_h(0)
         regroup_h(1, nc.vector.tensor_copy)
@@ -315,7 +318,7 @@ def tile_image_aggregation_pa_s_kernel(tc, h_cluster, w2c, b2c, scores, temperat
                     start=((i, c) == order[0]),
                     stop=((i, c) == order[-1]),
                 )
-                if by_half and (i, c) in ((2, 1), (2, 3), (2, 5)):
+                if by_half and (i, c) in ((2, 1), (2, 3)):
                     keep_clock(KEEP[4])
 
         def make_b(r):
@@ -344,20 +347,14 @@ def tile_image_aggregation_pa_s_kernel(tc, h_cluster, w2c, b2c, scores, temperat
         multiply_f(0)
         keep_clock(KEEP[5])
         make_b(0)
-        nc.vector.tensor_copy(out=bias_col[:], in_=spread_ps[:, 1, :])
-        nc.vector.reciprocal(out=inv_temp[:], in_=spread_ps[:, 0, 0:1])
+        nc.vector.tensor_copy(out=spread[:], in_=spread_ps[:])
         add_bias(0)
+        regroup_h(3, nc.scalar.copy, slice(N // 4, N // 2))
         quantise_h(1)
-        nc.vector.tensor_scalar_mul(out=neg_inv_temp[:], in0=inv_temp[:], scalar1=-1.0)
-        nc.vector.tensor_scalar_mul(
-            out=colmin_t[:].rearrange("p c b -> p (c b)"),
-            in0=colmin[:].rearrange("p c b -> p (c b)"),
-            scalar1=inv_temp[:, 0:1],
-        )
-        regroup_h(3, nc.vector.tensor_copy)
+        regroup_h(3, nc.vector.tensor_copy, slice(0, N // 4))
         sum_over_pixels(0)
-        multiply_f(1)
         keep_clock(KEEP[6])
+        multiply_f(1)
         turn_f(0)
         add_bias(1)
         make_a(0)
@@ -367,8 +364,7 @@ def tile_image_aggregation_pa_s_kernel(tc, h_cluster, w2c, b2c, scores, temperat
         multiply_f(2)
         keep_clock(KEEP[7])
         turn_f(1)
-        table_ready = keep.tile([P, 1], F32)
-        nc.scalar.activation(out=table_ready[:], in_=inv_temp[:], func=ACT.Ln)
+        nc.scalar.activation(out=table_ready[:], in_=first_sum[:], func=ACT.Ln)
         add_bias(2)
         make_b(1)
         quantise_h(3)
@@ -378,14 +374,20 @@ def tile_image_aggregation_pa_s_kernel(tc, h_cluster, w2c, b2c, scores, temperat
         keep_clock(KEEP[8])
         make_a(1)
         nc.vector.reduce_sum(out=a_col[:], in_=a_own[:], axis=AXIS_X)
+        nc.vector.reciprocal(out=inv_temp[:], in_=spread[:, 0, 0:1])
         quantise_f(0)
+        nc.vector.tensor_scalar_mul(out=neg_inv_temp[:], in0=inv_temp[:], scalar1=-1.0)
+        nc.vector.tensor_scalar_mul(
+            out=colmin_t[:].rearrange("p c b -> p (c b)"),
+            in0=colmin[:].rearrange("p c b -> p (c b)"),
+            scalar1=inv_temp[:, 0:1],
+        )
         ln_a_col = keep.tile([P, 1], F32)
         nc.scalar.activation(out=ln_a_col[:], in_=a_col[:], func=ACT.Ln)
         add_bias(3)
         log_ga = keep.tile([P, N], F32)
         log_ga_ps = {}
         sum_over_clusters(2)
-        keep_clock(KEEP[9])
         a_rows_ps = vecs.tile([P, BK], F32, tag="vec")
         nc.tensor.transpose(a_rows_ps[:], a_col[:, 0:1].to_broadcast([P, P]), ident[:])
         for g in range(PASSES):
@@ -399,6 +401,7 @@ def tile_image_aggregation_pa_s_kernel(tc, h_cluster, w2c, b2c, scores, temperat
             )
             log_ga_ps[g] = banks.tile([P, PACK, BK], F32, tag="bank", name="log_ga_ps%d" % g)
             turn_f(2 + g)
+            keep_clock(KEEP[9 + g])
             for t in range(PACK):
                 nc.tensor.transpose(log_ga_ps[g][:, t, :], log_ga[:, chunk_pixels(g * PACK + t)], ident[:])
         ga = keep.tile([P, CHUNKS, BK], F32)

@@ -24,7 +24,7 @@ HI, LO = 0, 1
 FAR = 2.0**120
 RUN = 4
 
-KEEP = (12, 3, 3, 6, 3, 4, 4, 4, 0, 2, 0)
+KEEP = (16, 0, 0, 4, 4, 4, 4, 4, 0, 0, 0)
 PRODUCT_CHUNKS = 6
 FLOPS = 2 * B * (D * HID * N + D * K * N)
 
@@ -100,12 +100,13 @@ def tile_image_aggregation_pa_s_kernel(tc, h_cluster, w2c, b2c, scores, temperat
         f_ps = {}
         f_turned_ps = {}
 
-        spare_ps = spare.tile([P, D], F32)
+        start_ps = spare.tile([P, PACK * D], F32)
+        spare_ps = start_ps[:, 0:D]
 
         def keep_clock(passes):
             for i in range(passes):
                 nc.tensor.matmul_mx(
-                    out=spare_ps[:],
+                    out=spare_ps,
                     lhsT=w_codes[:].bitcast(FP8X4),
                     lhsT_scale=w_scales[:],
                     rhs=w_codes[:].bitcast(FP8X4),
@@ -267,6 +268,7 @@ def tile_image_aggregation_pa_s_kernel(tc, h_cluster, w2c, b2c, scores, temperat
         turn(ps, 2, LO, 0)
         take(ps, 0, HI, 0, 1)
         take(ps, 2, LO, 0, 1)
+        nc.tensor.matmul(out=start_ps[:, 0:256], lhsT=ones_bf[:], rhs=s_rows[:, 0:256], start=True, stop=True)
         keep_clock(KEEP[1])
         ps = bank_of_pairs("pairs1")
         turn(ps, 0, HI, 1)
@@ -274,6 +276,7 @@ def tile_image_aggregation_pa_s_kernel(tc, h_cluster, w2c, b2c, scores, temperat
         turn(ps, 4, LO, 1)
         take(ps, 0, HI, 1, 2)
         take(ps, 4, LO, 1, 1)
+        nc.tensor.matmul(out=start_ps[:, 0:256], lhsT=ones_bf[:], rhs=s_rows[:, 0:256], start=True, stop=True)
         keep_clock(KEEP[2])
         ps = bank_of_pairs("pairs2")
         turn(ps, 0, HI, 3)

@@ -24,8 +24,8 @@ HI, LO = 0, 1
 FAR = 2.0**120
 RUN = 4
 
-KEEP = (16, 0, 0, 4, 4, 4, 4, 4, 0, 0, 0)
-PRODUCT_CHUNKS = 6
+KEEP = (12, 0, 0, 4, 4, 4, 4, 4, 0, 0, 0)
+PRODUCT_CHUNKS = 7
 FLOPS = 2 * B * (D * HID * N + D * K * N)
 
 
@@ -202,7 +202,6 @@ def tile_image_aggregation_pa_s_kernel(tc, h_cluster, w2c, b2c, scores, temperat
                 nc.tensor.transpose(d_cols_ps[k][:, t, :], d_rows[:, chunk_pixels(2 * k + t)], ident[:])
 
         colmin = keep.tile([P, CHUNKS, B], F32)
-        colmin_t = keep.tile([P, CHUNKS, B], F32)
         g_cols = keep.tile([P, CHUNKS, BK], F32)
         g_cols_pair = keep.tile([P, 2, CHUNKS, BK], BF16)
         g_rows_pair = keep.tile([P, 2, N], BF16)
@@ -225,9 +224,6 @@ def tile_image_aggregation_pa_s_kernel(tc, h_cluster, w2c, b2c, scores, temperat
         a_col = keep.tile([P, 1], F32)
         a_own = keep.tile([P, B], F32)
         a_pair = keep.tile([P, 2, B], BF16)
-        nc.vector.reciprocal(out=a_col[:], in_=first_sum[:])
-        nc.vector.tensor_scalar(out=a_pair[:, HI, :], in0=own_image[:], scalar1=a_col[:, 0:1], scalar2=None, op0=ALU.mult)
-        nc.vector.tensor_scalar(out=a_own[:], in0=own_image[:], scalar1=a_col[:, 0:1], scalar2=None, op0=ALU.mult)
         def make_high(k):
             chunks = slice(2 * k, 2 * k + 2)
             nc.vector.tensor_copy(out=g_cols_pair[:, HI, chunks, :], in_=g_cols[:, chunks, :])
@@ -255,11 +251,14 @@ def tile_image_aggregation_pa_s_kernel(tc, h_cluster, w2c, b2c, scores, temperat
             )
 
         make_high(0)
-        nc.vector.tensor_tensor(out=a_pair[:, LO, :], in0=a_own[:], in1=a_pair[:, HI, :], op=ALU.subtract)
+        nc.vector.reciprocal(out=a_col[:], in_=first_sum[:])
         make_low(0)
+        nc.vector.tensor_scalar(out=a_pair[:, HI, :], in0=own_image[:], scalar1=a_col[:, 0:1], scalar2=None, op0=ALU.mult)
+        nc.vector.tensor_scalar(out=a_own[:], in0=own_image[:], scalar1=a_col[:, 0:1], scalar2=None, op0=ALU.mult)
         make_high(1)
         make_high(2)
         make_low(1)
+        nc.vector.tensor_tensor(out=a_pair[:, LO, :], in0=a_own[:], in1=a_pair[:, HI, :], op=ALU.subtract)
         make_high(3)
         make_low(2)
         make_low(3)
@@ -289,17 +288,18 @@ def tile_image_aggregation_pa_s_kernel(tc, h_cluster, w2c, b2c, scores, temperat
         PRODUCTS = ((LO, HI), (HI, HI), (HI, LO))
         ctx.enter_context(nc.allow_low_precision("v[HI] is v rounded to bfloat16; v[LO] holds what that leaves"))
 
-        def reciprocal_pair(hi, lo, value, sums):
+        def reciprocal_pair(hi, lo, value, sums, meanwhile):
             nc.vector.reciprocal(out=hi, in_=sums)
             nc.vector.reciprocal(out=value, in_=sums)
+            meanwhile()
             nc.vector.tensor_tensor(out=lo, in0=value, in1=hi, op=ALU.subtract)
 
         inv_temp = keep.tile([P, 1], F32)
-        neg_inv_temp = keep.tile([P, 1], F32)
         spread = keep.tile([P, 2, 2], F32)
         regroup_h(0, nc.vector.tensor_copy)
+        regroup_h(1, nc.vector.tensor_copy, slice(0, N // 4))
         quantise_h(0)
-        regroup_h(1, nc.vector.tensor_copy)
+        regroup_h(1, nc.vector.tensor_copy, slice(N // 4, N // 2))
         regroup_h(2, nc.scalar.copy)
 
         b_vec = keep.tile([P, CHUNKS, B], F32)
@@ -307,7 +307,7 @@ def tile_image_aggregation_pa_s_kernel(tc, h_cluster, w2c, b2c, scores, temperat
         z_ps = {}
         y_ps = {}
 
-        def sum_over_clusters(r, by_half=False):
+        def sum_over_clusters(r, by_half=False, after={}):
             z_ps[r] = vecs.tile([P, CHUNKS, B], F32, tag="vec", name="z_ps%d" % r)
             order = [(i, c) for i in range(len(PRODUCTS)) for c in range(CHUNKS)]
             if by_half:
@@ -321,11 +321,11 @@ def tile_image_aggregation_pa_s_kernel(tc, h_cluster, w2c, b2c, scores, temperat
                     start=((i, c) == order[0]),
                     stop=((i, c) == order[-1]),
                 )
-                if by_half and (i, c) in ((2, 1), (2, 3)):
-                    keep_clock(KEEP[4])
+                if (i, c) in after:
+                    after[i, c]()
 
-        def make_b(r):
-            reciprocal_pair(b_pair[:, HI], b_pair[:, LO], b_vec[:], z_ps[r][:])
+        def make_b(r, meanwhile):
+            reciprocal_pair(b_pair[:, HI], b_pair[:, LO], b_vec[:], z_ps[r][:], meanwhile)
 
         def sum_over_pixels(r):
             y_ps[r] = vecs.tile([P, B], F32, tag="vec", name="y_ps%d" % r)
@@ -340,61 +340,59 @@ def tile_image_aggregation_pa_s_kernel(tc, h_cluster, w2c, b2c, scores, temperat
                         stop=(i == len(PRODUCTS) - 1 and c == CHUNKS - 1),
                     )
 
-        def make_a(r):
-            reciprocal_pair(a_pair[:, HI], a_pair[:, LO], a_own[:], y_ps[r][:])
+        def make_a(r, meanwhile):
+            reciprocal_pair(a_pair[:, HI], a_pair[:, LO], a_own[:], y_ps[r][:], meanwhile)
 
-        sum_over_clusters(0, by_half=True)
+        fill = lambda: keep_clock(KEEP[4])
+        sum_over_clusters(0, by_half=True, after={(2, 1): fill, (2, 3): fill})
         spread_ps = vecs.tile([P, 2, 2], F32, tag="vec")
         nc.tensor.matmul(out=spread_ps[:, 0, :], lhsT=ones_bf[:], rhs=row_bf[:, D : D + 2], start=True, stop=True)
         nc.tensor.matmul(out=spread_ps[:, 1, :], lhsT=row_bf[:, 0:D], rhs=ones_bf[:, 0:2], start=True, stop=True)
         multiply_f(0)
         keep_clock(KEEP[5])
-        make_b(0)
-        nc.vector.tensor_copy(out=spread[:], in_=spread_ps[:])
+        make_b(0, lambda: regroup_h(3, nc.vector.tensor_copy, slice(0, N // 8)))
+        nc.scalar.copy(out=spread[:], in_=spread_ps[:])
         add_bias(0)
         regroup_h(3, nc.scalar.copy, slice(N // 4, N // 2))
         quantise_h(1)
-        regroup_h(3, nc.vector.tensor_copy, slice(0, N // 4))
         sum_over_pixels(0)
         keep_clock(KEEP[6])
         multiply_f(1)
-        turn_f(0)
         add_bias(1)
-        make_a(0)
+        make_a(0, lambda: regroup_h(3, nc.vector.tensor_copy, slice(N // 8, N // 4)))
         quantise_h(2)
-        group_f(0, nc.vector.tensor_copy)
         sum_over_clusters(1)
+        turn_f(0)
         multiply_f(2)
         keep_clock(KEEP[7])
-        turn_f(1)
         nc.scalar.activation(out=table_ready[:], in_=first_sum[:], func=ACT.Ln)
         add_bias(2)
-        make_b(1)
+        make_b(1, lambda: group_f(0, nc.vector.tensor_copy))
         quantise_h(3)
-        group_f(1, nc.vector.tensor_copy)
         sum_over_pixels(1)
+        turn_f(1)
         multiply_f(3)
         keep_clock(KEEP[8])
-        make_a(1)
-        nc.vector.reduce_sum(out=a_col[:], in_=a_own[:], axis=AXIS_X)
+        def group_and_sum():
+            group_f(1, nc.vector.tensor_copy)
+            nc.vector.reduce_sum(out=a_col[:], in_=a_own[:], axis=AXIS_X)
+
+        make_a(1, group_and_sum)
         nc.vector.reciprocal(out=inv_temp[:], in_=spread[:, 0, 0:1])
         quantise_f(0)
-        nc.vector.tensor_scalar_mul(out=neg_inv_temp[:], in0=inv_temp[:], scalar1=-1.0)
-        nc.vector.tensor_scalar_mul(
-            out=colmin_t[:].rearrange("p c b -> p (c b)"),
-            in0=colmin[:].rearrange("p c b -> p (c b)"),
-            scalar1=inv_temp[:, 0:1],
-        )
         ln_a_col = keep.tile([P, 1], F32)
         nc.scalar.activation(out=ln_a_col[:], in_=a_col[:], func=ACT.Ln)
         add_bias(3)
         log_ga = keep.tile([P, N], F32)
         log_ga_ps = {}
-        sum_over_clusters(2)
         a_rows_ps = vecs.tile([P, BK], F32, tag="vec")
-        nc.tensor.transpose(a_rows_ps[:], a_col[:, 0:1].to_broadcast([P, P]), ident[:])
+
+        def spread_a():
+            nc.tensor.transpose(a_rows_ps[:], a_col[:, 0:1].to_broadcast([P, P]), ident[:])
+
+        sum_over_clusters(2, after={(1, CHUNKS - 1): spread_a})
         for g in range(PASSES):
-            nc.vector.tensor_scalar(
+            nc.gpsimd.tensor_scalar(
                 out=log_ga[:, pass_pixels(g)],
                 in0=d_rows[:, pass_pixels(g)],
                 scalar1=-1.0,
@@ -421,18 +419,13 @@ def tile_image_aggregation_pa_s_kernel(tc, h_cluster, w2c, b2c, scores, temperat
         ln_beta = keep.tile([P, CHUNKS, B], F32)
         plain = keep.tile([P, CHUNKS, BK], F32)
         tempered = keep.tile([P, CHUNKS, BK], F32)
-        nc.vector.scalar_tensor_tensor(
-            out=ln_beta[:].rearrange("p c b -> p (c b)"),
-            in0=ln_z[:].rearrange("p c b -> p (c b)"),
-            scalar=neg_inv_temp[:, 0:1],
-            in1=colmin_t[:].rearrange("p c b -> p (c b)"),
-            op0=ALU.mult,
-            op1=ALU.add,
-        )
-        nc.vector.reciprocal(out=b_vec[:], in_=z_ps[ROUNDS - 1][:])
         ln_b = keep.tile([P, CHUNKS, B], F32)
-        nc.vector.scalar_tensor_tensor(
-            out=ln_b[:], in0=ln_z[:], scalar=-1.0, in1=colmin[:], op0=ALU.mult, op1=ALU.add
+        nc.vector.tensor_tensor(out=ln_b[:], in0=colmin[:], in1=ln_z[:], op=ALU.subtract)
+        nc.vector.reciprocal(out=b_vec[:], in_=z_ps[ROUNDS - 1][:])
+        nc.vector.tensor_scalar_mul(
+            out=ln_beta[:].rearrange("p c b -> p (c b)"),
+            in0=ln_b[:].rearrange("p c b -> p (c b)"),
+            scalar1=inv_temp[:, 0:1],
         )
         for g in range(PASSES):
             for b in range(B):
@@ -452,16 +445,14 @@ def tile_image_aggregation_pa_s_kernel(tc, h_cluster, w2c, b2c, scores, temperat
                         bias=ln_b[:, c, b : b + 1],
                     )
         nc.scalar.activation(out=table_ready[:], in_=inv_temp[:], func=ACT.Abs_reciprocal_sqrt)
-        for chunks in (slice(0, PACK), slice(PACK, PRODUCT_CHUNKS)):
-            nc.vector.tensor_tensor(
-                out=by_image(plain[:, chunks, :]),
-                in0=by_image(ga[:, chunks, :]),
-                in1=b_vec[:, chunks, :].unsqueeze(3).to_broadcast([P, chunks.stop - chunks.start, B, K]),
-                op=ALU.mult,
-            )
+        nc.vector.tensor_tensor(
+            out=by_image(plain[:, 0:PRODUCT_CHUNKS, :]),
+            in0=by_image(ga[:, 0:PRODUCT_CHUNKS, :]),
+            in1=b_vec[:, 0:PRODUCT_CHUNKS, :].unsqueeze(3).to_broadcast([P, PRODUCT_CHUNKS, B, K]),
+            op=ALU.mult,
+        )
         group_f(2, nc.vector.tensor_copy)
         group_f(3, nc.vector.tensor_copy)
-        quantise_f(1)
 
         p_grouped = keep.tile([P, PASSES, BK, PACK], BF16, align_bytes=64)
         p_codes = keep.tile([P, PASSES, BK], U32, align_bytes=64)
@@ -471,14 +462,15 @@ def tile_image_aggregation_pa_s_kernel(tc, h_cluster, w2c, b2c, scores, temperat
             agg_ps[b] = banks.tile([P, BK], F32, tag="bank", name="agg_ps%d" % b)
         for g in range(PASSES):
             chunks = pass_chunks(g)
-            for b in range(B):
-                own = image_clusters(b)
+            for own in (slice(0, BK),) if g == 0 else (image_clusters(0), image_clusters(1)):
                 nc.vector.tensor_tensor(
                     out=p_grouped[:, g, own, :],
                     in0=plain[:, chunks, own].rearrange("p t m -> p m t"),
                     in1=tempered[:, chunks, own].rearrange("p t m -> p m t"),
                     op=ALU.add,
                 )
+            if g == 0:
+                quantise_f(1)
             nc.vector.quantize_mx(
                 out=p_codes[:, g, :].bitcast(FP8X4),
                 scales=p_scales[:, g, :],

from contextlib import ExitStack

import concourse.mybir as mybir
from concourse.masks import make_identity

F32 = mybir.dt.float32
BF16 = mybir.dt.bfloat16
U32 = mybir.dt.uint32
U8 = mybir.dt.uint8
FP8X4 = mybir.dt.float8_e4m3fn_x4
ALU = mybir.AluOpType
ACT = mybir.ActivationFunctionType
AXIS_X = mybir.AxisListType.X

P = 128
PACK = 4
B, HID, N, D, K = 2, 512, 1024, 128, 64
BK = B * K
CHUNKS = N // P
PASSES = N // (P * PACK)
PIECES = B * PASSES
ROUNDS = 3
HI, LO = 0, 1
FAR = 2.0**120
RUN = 4

KEEP = (12, 0, 0, 4, 4, 4, 4, 4, 0, 0, 0)
PRODUCT_CHUNKS = 7
FLOPS = 2 * B * (D * HID * N + D * K * N)


def pass_pixels(g):
    return slice(g * P * PACK, (g + 1) * P * PACK)


def pass_chunks(g):
    return slice(g * PACK, (g + 1) * PACK)


def chunk_pixels(c):
    return slice(c * P, (c + 1) * P)


def image_clusters(b):
    return slice(b * K, (b + 1) * K)


def by_image(cols):
    return cols.rearrange("p c (b k) -> p c b k", b=B)


def tile_image_aggregation_pa_s_kernel(tc, h_cluster, w2c, b2c, scores, temperature, out):
    nc = tc.nc
    with ExitStack() as ctx:
        ctx.enter_context(tc.manual_schedule())
        keep = ctx.enter_context(tc.tile_pool(name="keep", bufs=1))
        banks = ctx.enter_context(tc.psum_pool(name="banks", bufs=4))
        spare = ctx.enter_context(tc.psum_pool(name="spare", bufs=1))
        vecs = ctx.enter_context(tc.psum_pool(name="vecs", bufs=3))

        row_bf = keep.tile([P, D + 2], BF16)
        nc.vector.memset(row_bf[:], 0.0)
        ident = keep.tile([P, P], F32)
        make_identity(nc, ident[:])
        ident_bf = keep.tile([P, P], BF16)
        make_identity(nc, ident_bf[:])
        ones = keep.tile([P, P], F32)
        nc.gpsimd.memset(ones[:], 1.0)
        ones_bf = keep.tile([P, P], BF16)
        nc.gpsimd.memset(ones_bf[:], 1.0)
        own_image = keep.tile([P, B], F32)
        nc.vector.memset(own_image[:], 0.0)
        other_image = keep.tile([P, B], BF16)
        nc.vector.memset(other_image[:], FAR)
        for b in range(B):
            own = slice(b * K, (b + 1) * K)
            nc.vector.memset(own_image[own, b : b + 1], 1.0)
            nc.vector.memset(other_image[own, b : b + 1], 0.0)

        s_rows = keep.tile([P, N], BF16)
        nc.sync.dma_start(out=s_rows[:], in_=scores.rearrange("b k n -> (b k) n"))
        nc.scalar.dma_start(out=row_bf[0:1, 0:D], in_=b2c.unsqueeze(0))
        nc.scalar.dma_start(out=row_bf[0:1, D : D + 1], in_=temperature.unsqueeze(0))
        w_rows = keep.tile([P, HID], BF16)
        nc.sync.dma_start(out=w_rows[:], in_=w2c)
        h_raw = keep.tile([P, B, PACK, N], BF16)
        for b in range(B):
            nc.sync.dma_start(out=h_raw[:, b], in_=h_cluster[b].rearrange("(p j) n -> p j n", j=PACK))

        w_grouped = keep.tile([P, D * PACK], BF16, align_bytes=64)
        w_codes = keep.tile([P, D], U32, align_bytes=64)
        w_scales = keep.tile([P, D], U8, align_bytes=64)
        h_grouped = keep.tile([P, B, N, PACK], BF16, align_bytes=64)
        h_codes = keep.tile([P, B, N], U32, align_bytes=64)
        h_scales = keep.tile([P, B, N], U8, align_bytes=64)
        f_rows = keep.tile([P, PIECES, P * PACK], BF16, align_bytes=64)
        f_grouped = keep.tile([P, B, PASSES, D * PACK], BF16, align_bytes=64)
        f_codes = keep.tile([P, B, PASSES, D], U32, align_bytes=64)
        f_scales = keep.tile([P, B, PASSES, D], U8, align_bytes=64)
        f_ps = {}
        f_turned_ps = {}

        start_ps = spare.tile([P, PACK * D], F32)
        spare_ps = start_ps[:, 0:D]

        def keep_clock(passes):
            for i in range(passes):
                nc.tensor.matmul_mx(
                    out=spare_ps,
                    lhsT=w_codes[:].bitcast(FP8X4),
                    lhsT_scale=w_scales[:],
                    rhs=w_codes[:].bitcast(FP8X4),
                    rhs_scale=w_scales[:],
                    start=True,
                    stop=True,
                )

        def regroup_h(q, copy, part=slice(0, P * PACK)):
            b, g = q // PASSES, q % PASSES
            copy(
                out=h_grouped[:, b, pass_pixels(g), :][:, part, :].rearrange("p (c i) j -> p c j i", i=RUN),
                in_=h_raw[:, b, :, pass_pixels(g)][:, :, part].rearrange("p j (c i) -> p c j i", i=RUN),
            )

        def quantise_h(q):
            b, g = q // PASSES, q % PASSES
            nc.vector.quantize_mx(
                out=h_codes[:, b, pass_pixels(g)].bitcast(FP8X4),
                scales=h_scales[:, b, pass_pixels(g)],
                in_=h_grouped[:, b, pass_pixels(g), :].rearrange("p n j -> p (n j)"),
            )

        def multiply_f(q):
            b, g = q // PASSES, q % PASSES
            f_ps[q] = banks.tile([P, P * PACK], F32, tag="bank", name="f_ps%d" % q)
            nc.tensor.matmul_mx(
                out=f_ps[q][:],
                lhsT=w_codes[:].bitcast(FP8X4),
                lhsT_scale=w_scales[:],
                rhs=h_codes[:, b, pass_pixels(g)].bitcast(FP8X4),
                rhs_scale=h_scales[:, b, pass_pixels(g)],
                start=True,
                stop=True,
            )

        def add_bias(q):
            nc.scalar.activation(out=f_rows[:, q], in_=f_ps[q][:], func=ACT.Identity, bias=spread[:, 1, 0:1])

        def turn_f(q):
            f_turned_ps[q] = banks.tile([P, 2, D], F32, tag="bank", name="f_turned_ps%d" % q)
            words = f_rows[:, q].bitcast(F32)
            for u in range(2):
                nc.tensor.transpose(f_turned_ps[q][:, u, :], words[:, u * P : (u + 1) * P], ident[:])

        def group_f(q, copy):
            b, g = q // PASSES, q % PASSES
            copy(
                out=f_grouped[:, b, g].bitcast(F32).rearrange("p (d u) -> p d u", u=2),
                in_=f_turned_ps[q][:].rearrange("p u d -> p d u"),
            )

        def quantise_f(b):
            nc.vector.quantize_mx(
                out=f_codes[:, b].rearrange("p g d -> p (g d)").bitcast(FP8X4),
                scales=f_scales[:, b].rearrange("p g d -> p (g d)"),
                in_=f_grouped[:, b].rearrange("p g m -> p (g m)"),
            )

        table_ready = keep.tile([P, 1], F32)
        nc.scalar.activation(out=table_ready[:], in_=own_image[:, 0:1], func=ACT.Exp)
        rowmin = keep.tile([P, 1], F32)
        minus_s = keep.tile([P, N], BF16)
        nc.vector.tensor_scalar(
            out=minus_s[:], in0=s_rows[:], scalar1=-1.0, scalar2=None, op0=ALU.mult, op1=ALU.min, accum_out=rowmin[:]
        )
        exp_rows = keep.tile([P, N], BF16)
        first_sum = keep.tile([P, 1], F32)
        nc.scalar.activation(
            out=exp_rows[:], in_=s_rows[:], func=ACT.Exp, bias=rowmin[:, 0:1], accum_out=first_sum[:]
        )
        w_words = w_rows[:].bitcast(F32).rearrange("d (p u) -> d u p", u=2)
        w_ps = banks.tile([P, 2, D], F32, tag="bank")
        for u in range(2):
            nc.tensor.transpose(w_ps[:, u, :], w_words[:, u, :], ident[:])
        d_rows = keep.tile([P, N], F32)
        d_cols_ps = {}
        for k in range(CHUNKS // 2):
            quarter = slice(2 * k * P, (2 * k + 2) * P)
            nc.vector.tensor_scalar(
                out=d_rows[:, quarter].rearrange("p (e q) -> p e q", e=2),
                in0=minus_s[:, quarter].rearrange("p (q e) -> p e q", e=2),
                scalar1=rowmin[:, 0:1],
                scalar2=None,
                op0=ALU.subtract,
            )
        nc.vector.tensor_copy(
            out=w_grouped[:].bitcast(F32).rearrange("p (d u) -> p d u", u=2), in_=w_ps[:].rearrange("p u d -> p d u")
        )
        for k in range(CHUNKS // 2):
            d_cols_ps[k] = banks.tile([P, 2, BK], F32, tag="bank", name="d_cols_ps%d" % k)
            for t in range(2):
                nc.tensor.transpose(d_cols_ps[k][:, t, :], d_rows[:, chunk_pixels(2 * k + t)], ident[:])

        colmin = keep.tile([P, CHUNKS, B], F32)
        g_cols = keep.tile([P, CHUNKS, BK], F32)
        g_cols_pair = keep.tile([P, 2, CHUNKS, BK], BF16)
        g_rows_pair = keep.tile([P, 2, N], BF16)
        for k in range(CHUNKS // 2):
            nc.vector.tensor_reduce(
                out=colmin[:, 2 * k : 2 * k + 2, :], in_=by_image(d_cols_ps[k][:]), axis=AXIS_X, op=ALU.min
            )
            if k == 0:
                nc.vector.quantize_mx(out=w_codes[:].bitcast(FP8X4), scales=w_scales[:], in_=w_grouped[:])
                keep_clock(KEEP[0])
            for t in range(2):
                for b in range(B):
                    nc.scalar.activation(
                        out=g_cols[:, 2 * k + t, image_clusters(b)],
                        in_=d_cols_ps[k][:, t, image_clusters(b)],
                        func=ACT.Exp,
                        scale=-1.0,
                        bias=colmin[:, 2 * k + t, b : b + 1],
                    )
        a_col = keep.tile([P, 1], F32)
        a_own = keep.tile([P, B], F32)
        a_pair = keep.tile([P, 2, B], BF16)
        def make_high(k):
            chunks = slice(2 * k, 2 * k + 2)
            nc.vector.tensor_copy(out=g_cols_pair[:, HI, chunks, :], in_=g_cols[:, chunks, :])

        def make_low(k):
            chunks = slice(2 * k, 2 * k + 2)
            nc.vector.tensor_tensor(
                out=g_cols_pair[:, LO, chunks, :],
                in0=g_cols[:, chunks, :],
                in1=g_cols_pair[:, HI, chunks, :],
                op=ALU.subtract,
            )

        def turn(ps, at, part, k):
            for t in range(2):
                nc.tensor.transpose(ps[:, (at + t) * P : (at + t + 1) * P], g_cols_pair[:, part, 2 * k + t, :], ident_bf[:])

        def bank_of_pairs(name):
            return banks.tile([P, 6 * P], BF16, tag="bank", name=name)

        def take(ps, at, part, k, quarters):
            width = quarters * 2 * P
            nc.scalar.copy(
                out=g_rows_pair[:, part, k * 2 * P : k * 2 * P + width], in_=ps[:, at * P : at * P + width]
            )

        make_high(0)
        nc.vector.reciprocal(out=a_col[:], in_=first_sum[:])
        make_low(0)
        nc.vector.tensor_scalar(out=a_pair[:, HI, :], in0=own_image[:], scalar1=a_col[:, 0:1], scalar2=None, op0=ALU.mult)
        nc.vector.tensor_scalar(out=a_own[:], in0=own_image[:], scalar1=a_col[:, 0:1], scalar2=None, op0=ALU.mult)
        make_high(1)
        make_high(2)
        make_low(1)
        nc.vector.tensor_tensor(out=a_pair[:, LO, :], in0=a_own[:], in1=a_pair[:, HI, :], op=ALU.subtract)
        make_high(3)
        make_low(2)
        make_low(3)
        ps = bank_of_pairs("pairs0")
        turn(ps, 0, HI, 0)
        turn(ps, 2, LO, 0)
        take(ps, 0, HI, 0, 1)
        take(ps, 2, LO, 0, 1)
        nc.tensor.matmul(out=start_ps[:, 0:256], lhsT=ones_bf[:], rhs=s_rows[:, 0:256], start=True, stop=True)
        keep_clock(KEEP[1])
        ps = bank_of_pairs("pairs1")
        turn(ps, 0, HI, 1)
        turn(ps, 2, HI, 2)
        turn(ps, 4, LO, 1)
        take(ps, 0, HI, 1, 2)
        take(ps, 4, LO, 1, 1)
        nc.tensor.matmul(out=start_ps[:, 0:256], lhsT=ones_bf[:], rhs=s_rows[:, 0:256], start=True, stop=True)
        keep_clock(KEEP[2])
        ps = bank_of_pairs("pairs2")
        turn(ps, 0, HI, 3)
        turn(ps, 2, LO, 2)
        turn(ps, 4, LO, 3)
        take(ps, 0, HI, 3, 1)
        take(ps, 2, LO, 2, 2)
        keep_clock(KEEP[3])

        PRODUCTS = ((LO, HI), (HI, HI), (HI, LO))
        ctx.enter_context(nc.allow_low_precision("v[HI] is v rounded to bfloat16; v[LO] holds what that leaves"))

        def reciprocal_pair(hi, lo, value, sums, meanwhile):
            nc.vector.reciprocal(out=hi, in_=sums)
            nc.vector.reciprocal(out=value, in_=sums)
            meanwhile()
            nc.vector.tensor_tensor(out=lo, in0=value, in1=hi, op=ALU.subtract)

        inv_temp = keep.tile([P, 1], F32)
        spread = keep.tile([P, 2, 2], F32)
        regroup_h(0, nc.vector.tensor_copy)
        regroup_h(1, nc.vector.tensor_copy, slice(0, N // 4))
        quantise_h(0)
        regroup_h(1, nc.vector.tensor_copy, slice(N // 4, N // 2))
        regroup_h(2, nc.scalar.copy)

        b_vec = keep.tile([P, CHUNKS, B], F32)
        b_pair = keep.tile([P, 2, CHUNKS, B], BF16)
        z_ps = {}
        y_ps = {}

        def sum_over_clusters(r, by_half=False, after={}):
            z_ps[r] = vecs.tile([P, CHUNKS, B], F32, tag="vec", name="z_ps%d" % r)
            order = [(i, c) for i in range(len(PRODUCTS)) for c in range(CHUNKS)]
            if by_half:
                order.sort(key=lambda ic: ic[1] // 2)
            for i, c in order:
                g_part, v_part = PRODUCTS[i]
                nc.tensor.matmul(
                    out=z_ps[r][:, c, :],
                    lhsT=g_rows_pair[:, g_part, chunk_pixels(c)],
                    rhs=a_pair[:, v_part, :],
                    start=((i, c) == order[0]),
                    stop=((i, c) == order[-1]),
                )
                if (i, c) in after:
                    after[i, c]()

        def make_b(r, meanwhile):
            reciprocal_pair(b_pair[:, HI], b_pair[:, LO], b_vec[:], z_ps[r][:], meanwhile)

        def sum_over_pixels(r):
            y_ps[r] = vecs.tile([P, B], F32, tag="vec", name="y_ps%d" % r)
            nc.tensor.matmul(out=y_ps[r][:], lhsT=ident_bf[:], rhs=other_image[:], start=True, stop=False)
            for i, (g_part, v_part) in enumerate(PRODUCTS):
                for c in range(CHUNKS):
                    nc.tensor.matmul(
                        out=y_ps[r][:],
                        lhsT=g_cols_pair[:, g_part, c, :],
                        rhs=b_pair[:, v_part, c, :],
                        start=False,
                        stop=(i == len(PRODUCTS) - 1 and c == CHUNKS - 1),
                    )

        def make_a(r, meanwhile):
            reciprocal_pair(a_pair[:, HI], a_pair[:, LO], a_own[:], y_ps[r][:], meanwhile)

        fill = lambda: keep_clock(KEEP[4])
        sum_over_clusters(0, by_half=True, after={(2, 1): fill, (2, 3): fill})
        spread_ps = vecs.tile([P, 2, 2], F32, tag="vec")
        nc.tensor.matmul(out=spread_ps[:, 0, :], lhsT=ones_bf[:], rhs=row_bf[:, D : D + 2], start=True, stop=True)
        nc.tensor.matmul(out=spread_ps[:, 1, :], lhsT=row_bf[:, 0:D], rhs=ones_bf[:, 0:2], start=True, stop=True)
        multiply_f(0)
        keep_clock(KEEP[5])
        make_b(0, lambda: regroup_h(3, nc.vector.tensor_copy, slice(0, N // 8)))
        nc.scalar.copy(out=spread[:], in_=spread_ps[:])
        add_bias(0)
        regroup_h(3, nc.scalar.copy, slice(N // 4, N // 2))
        quantise_h(1)
        sum_over_pixels(0)
        keep_clock(KEEP[6])
        multiply_f(1)
        add_bias(1)
        make_a(0, lambda: regroup_h(3, nc.vector.tensor_copy, slice(N // 8, N // 4)))
        quantise_h(2)
        sum_over_clusters(1)
        turn_f(0)
        multiply_f(2)
        keep_clock(KEEP[7])
        nc.scalar.activation(out=table_ready[:], in_=first_sum[:], func=ACT.Ln)
        add_bias(2)
        make_b(1, lambda: group_f(0, nc.vector.tensor_copy))
        quantise_h(3)
        sum_over_pixels(1)
        turn_f(1)
        multiply_f(3)
        keep_clock(KEEP[8])
        def group_and_sum():
            group_f(1, nc.vector.tensor_copy)
            nc.vector.reduce_sum(out=a_col[:], in_=a_own[:], axis=AXIS_X)

        make_a(1, group_and_sum)
        nc.vector.reciprocal(out=inv_temp[:], in_=spread[:, 0, 0:1])
        quantise_f(0)
        ln_a_col = keep.tile([P, 1], F32)
        nc.scalar.activation(out=ln_a_col[:], in_=a_col[:], func=ACT.Ln)
        add_bias(3)
        log_ga = keep.tile([P, N], F32)
        log_ga_ps = {}
        a_rows_ps = vecs.tile([P, BK], F32, tag="vec")

        def spread_a():
            nc.tensor.transpose(a_rows_ps[:], a_col[:, 0:1].to_broadcast([P, P]), ident[:])

        sum_over_clusters(2, after={(1, CHUNKS - 1): spread_a})
        for g in range(PASSES):
            nc.gpsimd.tensor_scalar(
                out=log_ga[:, pass_pixels(g)],
                in0=d_rows[:, pass_pixels(g)],
                scalar1=-1.0,
                scalar2=ln_a_col[:, 0:1],
                op0=ALU.mult,
                op1=ALU.add,
            )
            log_ga_ps[g] = banks.tile([P, PACK, BK], F32, tag="bank", name="log_ga_ps%d" % g)
            turn_f(2 + g)
            keep_clock(KEEP[9 + g])
            for t in range(PACK):
                nc.tensor.transpose(log_ga_ps[g][:, t, :], log_ga[:, chunk_pixels(g * PACK + t)], ident[:])
        ga = keep.tile([P, CHUNKS, BK], F32)
        nc.vector.tensor_tensor(
            out=ga[:, 0:PRODUCT_CHUNKS, :],
            in0=g_cols[:, 0:PRODUCT_CHUNKS, :],
            in1=a_rows_ps[:].unsqueeze(1).to_broadcast([P, PRODUCT_CHUNKS, BK]),
            op=ALU.mult,
        )

        ln_z = keep.tile([P, CHUNKS, B], F32)
        nc.scalar.activation(out=ln_z[:], in_=z_ps[ROUNDS - 1][:], func=ACT.Ln)
        nc.scalar.activation(out=table_ready[:], in_=inv_temp[:], func=ACT.Exp)
        ln_beta = keep.tile([P, CHUNKS, B], F32)
        plain = keep.tile([P, CHUNKS, BK], F32)
        tempered = keep.tile([P, CHUNKS, BK], F32)
        ln_b = keep.tile([P, CHUNKS, B], F32)
        nc.vector.tensor_tensor(out=ln_b[:], in0=colmin[:], in1=ln_z[:], op=ALU.subtract)
        nc.vector.reciprocal(out=b_vec[:], in_=z_ps[ROUNDS - 1][:])
        nc.vector.tensor_scalar_mul(
            out=ln_beta[:].rearrange("p c b -> p (c b)"),
            in0=ln_b[:].rearrange("p c b -> p (c b)"),
            scalar1=inv_temp[:, 0:1],
        )
        for g in range(PASSES):
            for b in range(B):
                for c in range(g * PACK, (g + 1) * PACK):
                    nc.scalar.activation(
                        out=tempered[:, c, image_clusters(b)],
                        in_=log_ga_ps[g][:, c % PACK, image_clusters(b)],
                        func=ACT.Exp,
                        scale=inv_temp[:, 0:1],
                        bias=ln_beta[:, c, b : b + 1],
                    )
                for c in range(max(PRODUCT_CHUNKS, g * PACK), (g + 1) * PACK):
                    nc.scalar.activation(
                        out=plain[:, c, image_clusters(b)],
                        in_=log_ga_ps[g][:, c % PACK, image_clusters(b)],
                        func=ACT.Exp,
                        bias=ln_b[:, c, b : b + 1],
                    )
        nc.scalar.activation(out=table_ready[:], in_=inv_temp[:], func=ACT.Abs_reciprocal_sqrt)
        nc.vector.tensor_tensor(
            out=by_image(plain[:, 0:PRODUCT_CHUNKS, :]),
            in0=by_image(ga[:, 0:PRODUCT_CHUNKS, :]),
            in1=b_vec[:, 0:PRODUCT_CHUNKS, :].unsqueeze(3).to_broadcast([P, PRODUCT_CHUNKS, B, K]),
            op=ALU.mult,
        )
        group_f(2, nc.vector.tensor_copy)
        group_f(3, nc.vector.tensor_copy)

        p_grouped = keep.tile([P, PASSES, BK, PACK], BF16, align_bytes=64)
        p_codes = keep.tile([P, PASSES, BK], U32, align_bytes=64)
        p_scales = keep.tile([P, PASSES, BK], U8, align_bytes=64)
        agg_ps = {}
        for b in range(B):
            agg_ps[b] = banks.tile([P, BK], F32, tag="bank", name="agg_ps%d" % b)
        for g in range(PASSES):
            chunks = pass_chunks(g)
            for own in (slice(0, BK),) if g == 0 else (image_clusters(0), image_clusters(1)):
                nc.vector.tensor_tensor(
                    out=p_grouped[:, g, own, :],
                    in0=plain[:, chunks, own].rearrange("p t m -> p m t"),
                    in1=tempered[:, chunks, own].rearrange("p t m -> p m t"),
                    op=ALU.add,
                )
            if g == 0:
                quantise_f(1)
            nc.vector.quantize_mx(
                out=p_codes[:, g, :].bitcast(FP8X4),
                scales=p_scales[:, g, :],
                in_=p_grouped[:, g].rearrange("p m t -> p (m t)"),
            )
            for b in range(B):
                nc.tensor.matmul_mx(
                    out=agg_ps[b][:],
                    lhsT=f_codes[:, b, g, :].bitcast(FP8X4),
                    lhsT_scale=f_scales[:, b, g, :],
                    rhs=p_codes[:, g, :].bitcast(FP8X4),
                    rhs_scale=p_scales[:, g, :],
                    start=(g == 0),
                    stop=(g == PASSES - 1),
                )

        squares = keep.tile([P, B, K], F32)
        square_sums = keep.tile([P, B], F32)
        for b in range(B):
            nc.scalar.activation(
                out=squares[:, b, :],
                in_=agg_ps[b][:, b * K : (b + 1) * K],
                func=ACT.Square,
                accum_out=square_sums[:, b : b + 1],
            )
        total_ps = vecs.tile([P, B], F32, tag="vec")
        nc.tensor.matmul(out=total_ps[:], lhsT=ones[:], rhs=square_sums[:], start=True, stop=True)
        inv_norm = keep.tile([P, B], F32)
        nc.scalar.activation(out=inv_norm[:], in_=total_ps[:], func=ACT.Abs_reciprocal_sqrt)
        result = keep.tile([P, B, K], F32)
        for b in range(B):
            nc.vector.scalar_tensor_tensor(
                out=result[:, b, :],
                in0=inv_norm[:, b : b + 1].to_broadcast([P, K]),
                scalar=1e12,
                in1=agg_ps[b][:, b * K : (b + 1) * K],
                op0=ALU.min,
                op1=ALU.mult,
            )
        nc.sync.dma_start(out=out.rearrange("b (d k) -> d b k", k=K), in_=result[:])
